import numpy as np
import ml_dtypes


def mxq(x, axis, fmt="e4m3"):
    dtype, down = {"e4m3": (ml_dtypes.float8_e4m3fn, 7), "e5m2": (ml_dtypes.float8_e5m2, 14)}[fmt]
    v = np.moveaxis(np.asarray(x, np.float32).astype(ml_dtypes.bfloat16).astype(np.float64), axis, -1)
    blocks = v.reshape(v.shape[:-1] + (-1, 32))
    amax = np.abs(blocks).max(-1, keepdims=True)
    byte = np.maximum(np.where(amax > 0, np.frexp(amax)[1] - 1 + 127, 0) - down, 1)
    scale = np.exp2(byte - 127.0)
    codes = (blocks / scale).astype(np.float32).astype(dtype).astype(np.float64)
    return np.moveaxis((codes * scale).reshape(v.shape), -1, axis)


WIDE = False


def mx_kscale(k):
    if not WIDE:
        return np.ones(k)
    levels = np.array([10, -10, 5, -5, 0])
    a = np.random.permutation(np.resize(levels, k // 512 * 4)).reshape(k // 512, 4)
    idx = np.arange(k)
    return np.exp2(a[idx // 512, idx % 128 // 32])


BF16 = ml_dtypes.bfloat16


def bf(x):
    return np.asarray(x, np.float32).astype(BF16)


def f64(x):
    return np.asarray(x).astype(np.float64)


B, T, D, DEPTH, F = 2, 64, 512, 4, 64
L = 2 ** DEPTH
N = L - 1
LF = L * F


def sigmoid(v):
    return 1.0 / (1.0 + np.exp(-v))


def leaf_probs(c):
    probs = np.ones(c.shape[:-1] + (1,))
    for m in range(DEPTH):
        start = 2 ** m - 1
        cl = c[..., start:start + 2 ** m]
        probs = np.stack([probs * cl, probs * (1.0 - cl)], axis=-1)
        probs = probs.reshape(probs.shape[:-2] + (-1,))
    return probs


def setup_inputs():
    s = mx_kscale(D)
    t = mx_kscale(LF).reshape(L, F)
    return {"x": bf(np.random.standard_normal((B, T, D)) * s),
            "node_logits": bf(np.random.standard_normal((B, T, N)) * 1.5),
            "node_b": bf(np.random.standard_normal(N) * 0.5),
            "w1": bf(np.random.standard_normal((L, D, F)) / np.sqrt(D) / s[None, :, None] * t[:, None, :]),
            "b1": bf(np.random.standard_normal((L, F)) * 0.5 * t),
            "w2": bf(np.random.standard_normal((L, F, D)) * 2.0 / np.sqrt(F) / t[:, :, None])}


def reference(x, node_logits, node_b, w1, b1, w2):
    probs = leaf_probs(sigmoid(f64(node_logits) + f64(node_b)))
    w1f = f64(w1).transpose(1, 0, 2).reshape(D, LF)
    a = mxq(f64(x), 2, "e4m3") @ mxq(w1f, 0, "e4m3")
    h = np.maximum(a.reshape(B, T, L, F) + f64(b1), 0.0) * probs[..., None]
    return mxq(h.reshape(B, T, LF), 2, "e4m3") @ mxq(f64(w2).reshape(LF, D), 0, "e4m3")

@@ -1,0 +1,201 @@
+from contextlib import ExitStack
+
+import concourse.mybir as mybir
+from concourse.masks import make_identity
+
+BF16 = mybir.dt.bfloat16
+F32 = mybir.dt.float32
+U32 = mybir.dt.uint32
+U8 = mybir.dt.uint8
+FP8X4 = mybir.dt.float8_e4m3fn_x4
+ACT = mybir.ActivationFunctionType
+ALU = mybir.AluOpType
+
+P = 128
+PACK = 4
+K_PASS = P * PACK
+
+TOKENS = 128
+D = 512
+DEPTH = 4
+LEAVES = 2**DEPTH
+NODES = LEAVES - 1
+F = 64
+PASSES = LEAVES * F // K_PASS
+PASS_LEAVES = LEAVES // PASSES
+F_WORDS = F // PACK
+HALVES = 2
+E_HALF = D // HALVES
+
+FLOPS = 2 * TOKENS * D * LEAVES * F * 2
+
+
+def tile_fastfeedforwardnetwork_pa_s_kernel(tc, x, node_logits, node_b, w1, b1, w2, out):
+    nc = tc.nc
+    assert D == K_PASS and TOKENS == P
+    with ExitStack() as ctx:
+        keep = ctx.enter_context(tc.tile_pool(name="keep", bufs=1))
+        psum = ctx.enter_context(tc.psum_pool(name="psum", bufs=1))
+
+        x_rows = keep.tile([P, D], BF16)
+        nc.sync.dma_start(out=x_rows[:], in_=x.flatten_outer_dims())
+        logits = keep.tile([P, NODES], BF16)
+        nc.scalar.dma_start(out=logits[:], in_=node_logits.flatten_outer_dims())
+        node_bias = keep.tile([P, NODES], BF16)
+        nc.scalar.dma_start(out=node_bias[:], in_=node_b.partition_broadcast(P))
+        b1_cols = keep.tile([P, PASSES, PACK], BF16)
+        nc.scalar.dma_start(
+            out=b1_cols[:],
+            in_=b1.rearrange("l f -> (l f)").rearrange("(c m t) -> m c t", c=PASSES, t=PACK),
+        )
+        w1_raw = []
+        for c in range(PASSES):
+            raw = keep.tile([P, PASS_LEAVES, PACK * F], BF16, name="w1_raw%d" % c)
+            leaves = slice(c * PASS_LEAVES, (c + 1) * PASS_LEAVES)
+            nc.sync.dma_start(out=raw[:], in_=w1[leaves].rearrange("l (p j) f -> p l (j f)", j=PACK))
+            w1_raw.append(raw)
+        w2_rows = w2.rearrange("l f e -> (l f) e")
+        w2_raw = []
+        for c in range(PASSES):
+            raw = keep.tile([P, PACK, D], BF16, name="w2_raw%d" % c)
+            k_rows = slice(c * K_PASS, (c + 1) * K_PASS)
+            nc.sync.dma_start(out=raw[:], in_=w2_rows[k_rows].rearrange("(p t) e -> p t e", t=PACK))
+            w2_raw.append(raw)
+
+        identity = keep.tile([P, P], F32)
+        make_identity(nc, identity[:])
+
+        pre_gate = keep.tile([P, NODES], F32)
+        nc.vector.tensor_tensor(out=pre_gate[:], in0=logits[:], in1=node_bias[:], op=ALU.add)
+        gates = keep.tile([P, 2, NODES + 1], F32)
+        nc.scalar.activation(out=gates[:, 0, 0:NODES], in_=pre_gate[:], func=ACT.Sigmoid)
+        nc.vector.tensor_scalar(
+            out=gates[:, 1, 0:NODES], in0=gates[:, 0, 0:NODES], scalar1=-1.0, scalar2=1.0, op0=ALU.mult, op1=ALU.add
+        )
+        probs = gates[:, :, 0]
+        for level in range(1, DEPTH - 1):
+            count = 2**level
+            first = count - 1
+            children = keep.tile([P, count, 2], F32, name="probs%d" % level)
+            nc.vector.tensor_tensor(
+                out=children[:],
+                in0=probs.unsqueeze(2).to_broadcast([P, count, 2]),
+                in1=gates[:, :, first : first + count].rearrange("p s n -> p n s"),
+                op=ALU.mult,
+            )
+            probs = children[:].rearrange("p n s -> p (n s)")
+        count = LEAVES // 2
+        first = count - 1
+        leaf_probs = keep.tile([P, count, 2, F_WORDS], F32)
+        nc.vector.tensor_tensor(
+            out=leaf_probs[:],
+            in0=probs.unsqueeze(2).unsqueeze(3).to_broadcast([P, count, 2, F_WORDS]),
+            in1=gates[:, :, first : first + count]
+            .rearrange("p s n -> p n s")
+            .unsqueeze(3)
+            .to_broadcast([P, count, 2, F_WORDS]),
+            op=ALU.mult,
+        )
+        leaf_cols = leaf_probs[:].rearrange("p n s r -> p (n s r)")
+
+        x_words = x_rows[:].bitcast(F32).rearrange("r (p u) -> r u p", u=2)
+        x_t = psum.tile([P, 2, TOKENS], F32)
+        for u in range(2):
+            nc.tensor.transpose(out=x_t[:, u, :], in_=x_words[:, u, :], identity=identity[:])
+        probs_t = psum.tile([P, PASSES, TOKENS], F32)
+        for c in range(PASSES):
+            nc.tensor.transpose(out=probs_t[:, c, :], in_=leaf_cols[:, c * P : (c + 1) * P], identity=identity[:])
+
+        x_grouped = keep.tile([P, TOKENS * PACK], BF16, align_bytes=64)
+        nc.vector.tensor_copy(
+            out=x_grouped[:].bitcast(F32).rearrange("p (r u) -> p r u", u=2),
+            in_=x_t[:].rearrange("p u r -> p r u"),
+        )
+        x_codes = keep.tile([P, TOKENS], U32, align_bytes=64)
+        x_scales = keep.tile([P, TOKENS], U8, align_bytes=64)
+        nc.vector.quantize_mx(out=x_codes[:].bitcast(FP8X4), scales=x_scales[:], in_=x_grouped[:])
+
+        w1_codes = keep.tile([P, PASSES, PACK, P], U32, align_bytes=64)
+        w1_scales = keep.tile([P, PASSES, PACK, P], U8, align_bytes=64)
+        h_codes = keep.tile([P, PASSES, TOKENS], U32, align_bytes=64)
+        h_scales = keep.tile([P, PASSES, TOKENS], U8, align_bytes=64)
+        T_HALF = PACK // HALVES
+        for c in range(PASSES):
+            w1_grouped = keep.tile([P, PACK, P, PACK], BF16, name="w1_grouped%d" % c, align_bytes=64)
+            source = w1_raw[c][:].rearrange("p l (j f t) -> p t l f j", j=PACK, t=PACK)
+            target = w1_grouped[:].rearrange("p t (l f) j -> p t l f j", l=PASS_LEAVES)
+            nc.vector.tensor_copy(out=target[:, 0:T_HALF], in_=source[:, 0:T_HALF])
+            for t in range(T_HALF, PACK):
+                nc.scalar.copy(out=target[:, t], in_=source[:, t])
+            relu_h = keep.tile([P, PACK, TOKENS], F32, name="relu_h%d" % c)
+            for half in range(HALVES):
+                ts = slice(half * T_HALF, (half + 1) * T_HALF)
+                nc.vector.quantize_mx(
+                    out=w1_codes[:, c, ts, :].rearrange("p t m -> p (t m)").bitcast(FP8X4),
+                    scales=w1_scales[:, c, ts, :].rearrange("p t m -> p (t m)"),
+                    in_=w1_grouped[:, ts].rearrange("p t m j -> p (t m j)"),
+                )
+                pre_h = psum.tile([P, T_HALF, TOKENS], F32, name="pre_h%d_%d" % (c, half))
+                for i in range(T_HALF):
+                    t = half * T_HALF + i
+                    nc.tensor.matmul_mx(
+                        out=pre_h[:, i, :],
+                        lhsT=w1_codes[:, c, t, :].bitcast(FP8X4),
+                        lhsT_scale=w1_scales[:, c, t, :],
+                        rhs=x_codes[:].bitcast(FP8X4),
+                        rhs_scale=x_scales[:],
+                        start=True,
+                        stop=True,
+                    )
+                for i in range(T_HALF):
+                    t = half * T_HALF + i
+                    nc.scalar.activation(
+                        out=relu_h[:, t, :], in_=pre_h[:, i, :], func=ACT.Relu, bias=b1_cols[:, c, t : t + 1], scale=1.0
+                    )
+            h_grouped = keep.tile([P, TOKENS, PACK], BF16, name="h_grouped%d" % c, align_bytes=64)
+            nc.vector.tensor_tensor(
+                out=h_grouped[:],
+                in0=relu_h[:].rearrange("p t r -> p r t"),
+                in1=probs_t[:, c, :].unsqueeze(2).to_broadcast([P, TOKENS, PACK]),
+                op=ALU.mult,
+            )
+            nc.vector.quantize_mx(
+                out=h_codes[:, c, :].bitcast(FP8X4),
+                scales=h_scales[:, c, :],
+                in_=h_grouped[:].rearrange("p r t -> p (r t)"),
+            )
+
+        w2_codes = keep.tile([P, PASSES, D], U32, align_bytes=64)
+        w2_scales = keep.tile([P, PASSES, D], U8, align_bytes=64)
+        out_ps = [psum.tile([P, E_HALF], F32, name="out_ps%d" % half) for half in range(HALVES)]
+        for c in range(PASSES):
+            w2_grouped = keep.tile([P, D, PACK], BF16, name="w2_grouped%d" % c, align_bytes=64)
+            source = w2_raw[c][:].rearrange("p t (g i) -> p g t i", i=4)
+            target = w2_grouped[:].rearrange("p (g i) t -> p g t i", i=4)
+            groups = E_HALF // 4
+            nc.vector.tensor_copy(out=target[:, 0:groups], in_=source[:, 0:groups])
+            nc.scalar.copy(out=target[:, groups : 2 * groups], in_=source[:, groups : 2 * groups])
+            for half in range(HALVES):
+                e_cols = slice(half * E_HALF, (half + 1) * E_HALF)
+                nc.vector.quantize_mx(
+                    out=w2_codes[:, c, e_cols].bitcast(FP8X4),
+                    scales=w2_scales[:, c, e_cols],
+                    in_=w2_grouped[:, e_cols, :].rearrange("p e t -> p (e t)"),
+                )
+                nc.tensor.matmul_mx(
+                    out=out_ps[half][:],
+                    lhsT=h_codes[:, c, :].bitcast(FP8X4),
+                    lhsT_scale=h_scales[:, c, :],
+                    rhs=w2_codes[:, c, e_cols].bitcast(FP8X4),
+                    rhs_scale=w2_scales[:, c, e_cols],
+                    start=(c == 0),
+                    stop=(c == PASSES - 1),
+                )
+
+        out_rows = out.flatten_outer_dims()
+        result0 = keep.tile([P, E_HALF], F32)
+        nc.vector.tensor_copy(out=result0[:], in_=out_ps[0][:])
+        nc.sync.dma_start(out=out_rows[:, 0:E_HALF], in_=result0[:])
+        result1 = keep.tile([P, E_HALF], F32)
+        nc.scalar.copy(out=result1[:], in_=out_ps[1][:])
+        nc.sync.dma_start(out=out_rows[:, E_HALF:D], in_=result1[:])

@@ -26,6 +26,7 @@ PASS_LEAVES = LEAVES // PASSES
 F_WORDS = F // PACK
 HALVES = 2
 E_HALF = D // HALVES
+T_HALF = PACK // HALVES
 
 FLOPS = 2 * TOKENS * D * LEAVES * F * 2
 
@@ -36,6 +37,7 @@ def tile_fastfeedforwardnetwork_pa_s_kernel(tc, x, node_logits, node_b, w1, b1, 
     with ExitStack() as ctx:
         keep = ctx.enter_context(tc.tile_pool(name="keep", bufs=1))
         psum = ctx.enter_context(tc.psum_pool(name="psum", bufs=1))
+        ctx.enter_context(tc.manual_schedule())
 
         x_rows = keep.tile([P, D], BF16)
         nc.sync.dma_start(out=x_rows[:], in_=x.flatten_outer_dims())
@@ -117,80 +119,110 @@ def tile_fastfeedforwardnetwork_pa_s_kernel(tc, x, node_logits, node_b, w1, b1, 
 
         w1_codes = keep.tile([P, PASSES, PACK, P], U32, align_bytes=64)
         w1_scales = keep.tile([P, PASSES, PACK, P], U8, align_bytes=64)
+        w1_grouped = [
+            keep.tile([P, PACK, P, PACK], BF16, name="w1_grouped%d" % c, align_bytes=64) for c in range(PASSES)
+        ]
+        relu_h = [keep.tile([P, PACK, TOKENS], F32, name="relu_h%d" % c) for c in range(PASSES)]
+        h_grouped = [keep.tile([P, TOKENS, PACK], BF16, name="h_grouped%d" % c, align_bytes=64) for c in range(PASSES)]
         h_codes = keep.tile([P, PASSES, TOKENS], U32, align_bytes=64)
         h_scales = keep.tile([P, PASSES, TOKENS], U8, align_bytes=64)
-        T_HALF = PACK // HALVES
-        for c in range(PASSES):
-            w1_grouped = keep.tile([P, PACK, P, PACK], BF16, name="w1_grouped%d" % c, align_bytes=64)
+        w2_codes = keep.tile([P, PASSES, D], U32, align_bytes=64)
+        w2_scales = keep.tile([P, PASSES, D], U8, align_bytes=64)
+        w2_grouped = [keep.tile([P, D, PACK], BF16, name="w2_grouped%d" % c, align_bytes=64) for c in range(PASSES)]
+        out_ps = [psum.tile([P, E_HALF], F32, name="out_ps%d" % half) for half in range(HALVES)]
+
+        def regroup_w1(c):
             source = w1_raw[c][:].rearrange("p l (j f t) -> p t l f j", j=PACK, t=PACK)
-            target = w1_grouped[:].rearrange("p t (l f) j -> p t l f j", l=PASS_LEAVES)
+            target = w1_grouped[c][:].rearrange("p t (l f) j -> p t l f j", l=PASS_LEAVES)
             nc.vector.tensor_copy(out=target[:, 0:T_HALF], in_=source[:, 0:T_HALF])
             for t in range(T_HALF, PACK):
                 nc.scalar.copy(out=target[:, t], in_=source[:, t])
-            relu_h = keep.tile([P, PACK, TOKENS], F32, name="relu_h%d" % c)
-            for half in range(HALVES):
-                ts = slice(half * T_HALF, (half + 1) * T_HALF)
-                nc.vector.quantize_mx(
-                    out=w1_codes[:, c, ts, :].rearrange("p t m -> p (t m)").bitcast(FP8X4),
-                    scales=w1_scales[:, c, ts, :].rearrange("p t m -> p (t m)"),
-                    in_=w1_grouped[:, ts].rearrange("p t m j -> p (t m j)"),
+
+        def hidden_products(c, half):
+            ts = slice(half * T_HALF, (half + 1) * T_HALF)
+            nc.vector.quantize_mx(
+                out=w1_codes[:, c, ts, :].rearrange("p t m -> p (t m)").bitcast(FP8X4),
+                scales=w1_scales[:, c, ts, :].rearrange("p t m -> p (t m)"),
+                in_=w1_grouped[c][:, ts].rearrange("p t m j -> p (t m j)"),
+            )
+            pre_h = psum.tile([P, T_HALF, TOKENS], F32, name="pre_h%d_%d" % (c, half))
+            for i in range(T_HALF):
+                t = half * T_HALF + i
+                nc.tensor.matmul_mx(
+                    out=pre_h[:, i, :],
+                    lhsT=w1_codes[:, c, t, :].bitcast(FP8X4),
+                    lhsT_scale=w1_scales[:, c, t, :],
+                    rhs=x_codes[:].bitcast(FP8X4),
+                    rhs_scale=x_scales[:],
+                    start=True,
+                    stop=True,
                 )
-                pre_h = psum.tile([P, T_HALF, TOKENS], F32, name="pre_h%d_%d" % (c, half))
-                for i in range(T_HALF):
-                    t = half * T_HALF + i
-                    nc.tensor.matmul_mx(
-                        out=pre_h[:, i, :],
-                        lhsT=w1_codes[:, c, t, :].bitcast(FP8X4),
-                        lhsT_scale=w1_scales[:, c, t, :],
-                        rhs=x_codes[:].bitcast(FP8X4),
-                        rhs_scale=x_scales[:],
-                        start=True,
-                        stop=True,
-                    )
-                for i in range(T_HALF):
-                    t = half * T_HALF + i
-                    nc.scalar.activation(
-                        out=relu_h[:, t, :], in_=pre_h[:, i, :], func=ACT.Relu, bias=b1_cols[:, c, t : t + 1], scale=1.0
-                    )
-            h_grouped = keep.tile([P, TOKENS, PACK], BF16, name="h_grouped%d" % c, align_bytes=64)
+            for i in range(T_HALF):
+                t = half * T_HALF + i
+                nc.scalar.activation(
+                    out=relu_h[c][:, t, :], in_=pre_h[:, i, :], func=ACT.Relu, bias=b1_cols[:, c, t : t + 1], scale=1.0
+                )
+
+        def weight_hidden(c):
             nc.vector.tensor_tensor(
-                out=h_grouped[:],
-                in0=relu_h[:].rearrange("p t r -> p r t"),
+                out=h_grouped[c][:],
+                in0=relu_h[c][:].rearrange("p t r -> p r t"),
                 in1=probs_t[:, c, :].unsqueeze(2).to_broadcast([P, TOKENS, PACK]),
                 op=ALU.mult,
             )
+
+        def quantise_hidden(c):
             nc.vector.quantize_mx(
                 out=h_codes[:, c, :].bitcast(FP8X4),
                 scales=h_scales[:, c, :],
-                in_=h_grouped[:].rearrange("p r t -> p (r t)"),
+                in_=h_grouped[c][:].rearrange("p r t -> p (r t)"),
             )
 
-        w2_codes = keep.tile([P, PASSES, D], U32, align_bytes=64)
-        w2_scales = keep.tile([P, PASSES, D], U8, align_bytes=64)
-        out_ps = [psum.tile([P, E_HALF], F32, name="out_ps%d" % half) for half in range(HALVES)]
-        for c in range(PASSES):
-            w2_grouped = keep.tile([P, D, PACK], BF16, name="w2_grouped%d" % c, align_bytes=64)
+        def regroup_w2(c):
             source = w2_raw[c][:].rearrange("p t (g i) -> p g t i", i=4)
-            target = w2_grouped[:].rearrange("p (g i) t -> p g t i", i=4)
+            target = w2_grouped[c][:].rearrange("p (g i) t -> p g t i", i=4)
             groups = E_HALF // 4
             nc.vector.tensor_copy(out=target[:, 0:groups], in_=source[:, 0:groups])
             nc.scalar.copy(out=target[:, groups : 2 * groups], in_=source[:, groups : 2 * groups])
-            for half in range(HALVES):
-                e_cols = slice(half * E_HALF, (half + 1) * E_HALF)
-                nc.vector.quantize_mx(
-                    out=w2_codes[:, c, e_cols].bitcast(FP8X4),
-                    scales=w2_scales[:, c, e_cols],
-                    in_=w2_grouped[:, e_cols, :].rearrange("p e t -> p (e t)"),
-                )
-                nc.tensor.matmul_mx(
-                    out=out_ps[half][:],
-                    lhsT=h_codes[:, c, :].bitcast(FP8X4),
-                    lhsT_scale=h_scales[:, c, :],
-                    rhs=w2_codes[:, c, e_cols].bitcast(FP8X4),
-                    rhs_scale=w2_scales[:, c, e_cols],
-                    start=(c == 0),
-                    stop=(c == PASSES - 1),
-                )
+
+        def quantise_w2(c, half):
+            e_cols = slice(half * E_HALF, (half + 1) * E_HALF)
+            nc.vector.quantize_mx(
+                out=w2_codes[:, c, e_cols].bitcast(FP8X4),
+                scales=w2_scales[:, c, e_cols],
+                in_=w2_grouped[c][:, e_cols, :].rearrange("p e t -> p (e t)"),
+            )
+
+        def output_product(c, half):
+            e_cols = slice(half * E_HALF, (half + 1) * E_HALF)
+            nc.tensor.matmul_mx(
+                out=out_ps[half][:],
+                lhsT=h_codes[:, c, :].bitcast(FP8X4),
+                lhsT_scale=h_scales[:, c, :],
+                rhs=w2_codes[:, c, e_cols].bitcast(FP8X4),
+                rhs_scale=w2_scales[:, c, e_cols],
+                start=(c == 0),
+                stop=(c == PASSES - 1),
+            )
+
+        regroup_w1(0)
+        for c in range(PASSES):
+            hidden_products(c, 0)
+            if c + 1 < PASSES:
+                regroup_w1(c + 1)
+            else:
+                regroup_w2(0)
+            hidden_products(c, 1)
+
+        for c in range(PASSES):
+            weight_hidden(c)
+            quantise_w2(c, 0)
+            quantise_hidden(c)
+            output_product(c, 0)
+            if c + 1 < PASSES:
+                regroup_w2(c + 1)
+            quantise_w2(c, 1)
+            output_product(c, 1)
 
         out_rows = out.flatten_outer_dims()
         result0 = keep.tile([P, E_HALF], F32)

@@ -20,6 +20,7 @@ D = 512
 DEPTH = 4
 LEAVES = 2**DEPTH
 NODES = LEAVES - 1
+NODE_COLS = 32
 F = 64
 PASSES = LEAVES * F // K_PASS
 PASS_LEAVES = LEAVES // PASSES
@@ -37,14 +38,18 @@ def tile_fastfeedforwardnetwork_pa_s_kernel(tc, x, node_logits, node_b, w1, b1, 
     with ExitStack() as ctx:
         keep = ctx.enter_context(tc.tile_pool(name="keep", bufs=1))
         psum = ctx.enter_context(tc.psum_pool(name="psum", bufs=1))
+        psum_h = ctx.enter_context(tc.psum_pool(name="psum_h", bufs=2))
         ctx.enter_context(tc.manual_schedule())
 
         x_rows = keep.tile([P, D], BF16)
         nc.sync.dma_start(out=x_rows[:], in_=x.flatten_outer_dims())
         logits = keep.tile([P, NODES], BF16)
         nc.scalar.dma_start(out=logits[:], in_=node_logits.flatten_outer_dims())
-        node_bias = keep.tile([P, NODES], BF16)
-        nc.scalar.dma_start(out=node_bias[:], in_=node_b.partition_broadcast(P))
+        node_b_row = keep.tile([P, NODE_COLS], BF16)
+        nc.gpsimd.memset(node_b_row[:], 0.0)
+        nc.scalar.dma_start(out=node_b_row[0:1, 0:NODES], in_=node_b.rearrange("(o n) -> o n", o=1))
+        ones = keep.tile([P, P], BF16)
+        nc.gpsimd.memset(ones[:], 1.0)
         b1_cols = keep.tile([P, PASSES, PACK], BF16)
         nc.scalar.dma_start(
             out=b1_cols[:],
@@ -68,7 +73,9 @@ def tile_fastfeedforwardnetwork_pa_s_kernel(tc, x, node_logits, node_b, w1, b1, 
         make_identity(nc, identity[:])
 
         pre_gate = keep.tile([P, NODES], F32)
-        nc.vector.tensor_tensor(out=pre_gate[:], in0=logits[:], in1=node_bias[:], op=ALU.add)
+        node_bias = psum.tile([P, NODE_COLS], F32)
+        nc.tensor.matmul(out=node_bias[:], lhsT=ones[:], rhs=node_b_row[:], start=True, stop=True)
+        nc.vector.tensor_tensor(out=pre_gate[:], in0=logits[:], in1=node_bias[:, 0:NODES], op=ALU.add)
         gates = keep.tile([P, 2, NODES + 1], F32)
         nc.scalar.activation(out=gates[:, 0, 0:NODES], in_=pre_gate[:], func=ACT.Sigmoid)
         nc.vector.tensor_scalar(
@@ -145,7 +152,7 @@ def tile_fastfeedforwardnetwork_pa_s_kernel(tc, x, node_logits, node_b, w1, b1, 
                 scales=w1_scales[:, c, ts, :].rearrange("p t m -> p (t m)"),
                 in_=w1_grouped[c][:, ts].rearrange("p t m j -> p (t m j)"),
             )
-            pre_h = psum.tile([P, T_HALF, TOKENS], F32, name="pre_h%d_%d" % (c, half))
+            pre_h = psum_h.tile([P, T_HALF, TOKENS], F32)
             for i in range(T_HALF):
                 t = half * T_HALF + i
                 nc.tensor.matmul_mx(

@@ -17,10 +17,8 @@ K_PASS = P * PACK
 
 TOKENS = 128
 D = 512
-DEPTH = 4
-LEAVES = 2**DEPTH
+LEAVES = 16
 NODES = LEAVES - 1
-NODE_COLS = 32
 F = 64
 PASSES = LEAVES * F // K_PASS
 PASS_LEAVES = LEAVES // PASSES
@@ -28,6 +26,7 @@ F_WORDS = F // PACK
 HALVES = 2
 E_HALF = D // HALVES
 T_HALF = PACK // HALVES
+LOAD_LEAVES = PASS_LEAVES // HALVES
 
 FLOPS = 2 * TOKENS * D * LEAVES * F * 2
 
@@ -38,109 +37,64 @@ def tile_fastfeedforwardnetwork_pa_s_kernel(tc, x, node_logits, node_b, w1, b1, 
     with ExitStack() as ctx:
         keep = ctx.enter_context(tc.tile_pool(name="keep", bufs=1))
         psum = ctx.enter_context(tc.psum_pool(name="psum", bufs=1))
-        psum_h = ctx.enter_context(tc.psum_pool(name="psum_h", bufs=2))
         ctx.enter_context(tc.manual_schedule())
 
+        logits = keep.tile([P, NODES], BF16)
+        nc.sync.dma_start(out=logits[:], in_=node_logits.flatten_outer_dims())
+        node_bias = keep.tile([P, NODES], BF16)
+        nc.sync.dma_start(out=node_bias[:], in_=node_b.partition_broadcast(P))
         x_rows = keep.tile([P, D], BF16)
         nc.sync.dma_start(out=x_rows[:], in_=x.flatten_outer_dims())
-        logits = keep.tile([P, NODES], BF16)
-        nc.scalar.dma_start(out=logits[:], in_=node_logits.flatten_outer_dims())
-        node_b_row = keep.tile([P, NODE_COLS], BF16)
-        nc.gpsimd.memset(node_b_row[:], 0.0)
-        nc.scalar.dma_start(out=node_b_row[0:1, 0:NODES], in_=node_b.rearrange("(o n) -> o n", o=1))
-        ones = keep.tile([P, P], BF16)
-        nc.gpsimd.memset(ones[:], 1.0)
+        w1_raw = [
+            [keep.tile([P, LOAD_LEAVES, PACK * F], BF16, name="w1_raw%d_%d" % (c, part)) for part in range(HALVES)]
+            for c in range(PASSES)
+        ]
+        for c in range(PASSES):
+            for part in range(HALVES):
+                first = c * PASS_LEAVES + part * LOAD_LEAVES
+                nc.sync.dma_start(
+                    out=w1_raw[c][part][:],
+                    in_=w1[first : first + LOAD_LEAVES].rearrange("l (p j) f -> p l (j f)", j=PACK),
+                )
+        w2_rows = w2.rearrange("l f e -> (l f) e")
+        w2_raw = [keep.tile([P, PACK, D], BF16, name="w2_raw%d" % c) for c in range(PASSES)]
+        for c in range(PASSES):
+            k_rows = slice(c * K_PASS, (c + 1) * K_PASS)
+            nc.sync.dma_start(out=w2_raw[c][:], in_=w2_rows[k_rows].rearrange("(p t) e -> p t e", t=PACK))
         b1_cols = keep.tile([P, PASSES, PACK], BF16)
         nc.scalar.dma_start(
             out=b1_cols[:],
             in_=b1.rearrange("l f -> (l f)").rearrange("(c m t) -> m c t", c=PASSES, t=PACK),
         )
-        w1_raw = []
-        for c in range(PASSES):
-            raw = keep.tile([P, PASS_LEAVES, PACK * F], BF16, name="w1_raw%d" % c)
-            leaves = slice(c * PASS_LEAVES, (c + 1) * PASS_LEAVES)
-            nc.sync.dma_start(out=raw[:], in_=w1[leaves].rearrange("l (p j) f -> p l (j f)", j=PACK))
-            w1_raw.append(raw)
-        w2_rows = w2.rearrange("l f e -> (l f) e")
-        w2_raw = []
-        for c in range(PASSES):
-            raw = keep.tile([P, PACK, D], BF16, name="w2_raw%d" % c)
-            k_rows = slice(c * K_PASS, (c + 1) * K_PASS)
-            nc.sync.dma_start(out=raw[:], in_=w2_rows[k_rows].rearrange("(p t) e -> p t e", t=PACK))
-            w2_raw.append(raw)
 
         identity = keep.tile([P, P], F32)
         make_identity(nc, identity[:])
 
-        pre_gate = keep.tile([P, NODES], F32)
-        node_bias = psum.tile([P, NODE_COLS], F32)
-        nc.tensor.matmul(out=node_bias[:], lhsT=ones[:], rhs=node_b_row[:], start=True, stop=True)
-        nc.vector.tensor_tensor(out=pre_gate[:], in0=logits[:], in1=node_bias[:, 0:NODES], op=ALU.add)
-        gates = keep.tile([P, 2, NODES + 1], F32)
-        nc.scalar.activation(out=gates[:, 0, 0:NODES], in_=pre_gate[:], func=ACT.Sigmoid)
-        nc.vector.tensor_scalar(
-            out=gates[:, 1, 0:NODES], in0=gates[:, 0, 0:NODES], scalar1=-1.0, scalar2=1.0, op0=ALU.mult, op1=ALU.add
-        )
-        probs = gates[:, :, 0]
-        for level in range(1, DEPTH - 1):
-            count = 2**level
-            first = count - 1
-            children = keep.tile([P, count, 2], F32, name="probs%d" % level)
-            nc.vector.tensor_tensor(
-                out=children[:],
-                in0=probs.unsqueeze(2).to_broadcast([P, count, 2]),
-                in1=gates[:, :, first : first + count].rearrange("p s n -> p n s"),
-                op=ALU.mult,
-            )
-            probs = children[:].rearrange("p n s -> p (n s)")
-        count = LEAVES // 2
-        first = count - 1
-        leaf_probs = keep.tile([P, count, 2, F_WORDS], F32)
-        nc.vector.tensor_tensor(
-            out=leaf_probs[:],
-            in0=probs.unsqueeze(2).unsqueeze(3).to_broadcast([P, count, 2, F_WORDS]),
-            in1=gates[:, :, first : first + count]
-            .rearrange("p s n -> p n s")
-            .unsqueeze(3)
-            .to_broadcast([P, count, 2, F_WORDS]),
-            op=ALU.mult,
-        )
-        leaf_cols = leaf_probs[:].rearrange("p n s r -> p (n s r)")
-
-        x_words = x_rows[:].bitcast(F32).rearrange("r (p u) -> r u p", u=2)
-        x_t = psum.tile([P, 2, TOKENS], F32)
-        for u in range(2):
-            nc.tensor.transpose(out=x_t[:, u, :], in_=x_words[:, u, :], identity=identity[:])
-        probs_t = psum.tile([P, PASSES, TOKENS], F32)
-        for c in range(PASSES):
-            nc.tensor.transpose(out=probs_t[:, c, :], in_=leaf_cols[:, c * P : (c + 1) * P], identity=identity[:])
-
         x_grouped = keep.tile([P, TOKENS * PACK], BF16, align_bytes=64)
-        nc.vector.tensor_copy(
-            out=x_grouped[:].bitcast(F32).rearrange("p (r u) -> p r u", u=2),
-            in_=x_t[:].rearrange("p u r -> p r u"),
-        )
         x_codes = keep.tile([P, TOKENS], U32, align_bytes=64)
         x_scales = keep.tile([P, TOKENS], U8, align_bytes=64)
-        nc.vector.quantize_mx(out=x_codes[:].bitcast(FP8X4), scales=x_scales[:], in_=x_grouped[:])
-
-        w1_codes = keep.tile([P, PASSES, PACK, P], U32, align_bytes=64)
-        w1_scales = keep.tile([P, PASSES, PACK, P], U8, align_bytes=64)
         w1_grouped = [
             keep.tile([P, PACK, P, PACK], BF16, name="w1_grouped%d" % c, align_bytes=64) for c in range(PASSES)
+        ]
+        w1_codes = keep.tile([P, PASSES, PACK, P], U32, align_bytes=64)
+        w1_scales = keep.tile([P, PASSES, PACK, P], U8, align_bytes=64)
+        pre_h = [
+            [psum.tile([P, T_HALF, TOKENS], F32, name="pre_h%d_%d" % (c, half)) for half in range(HALVES)]
+            for c in range(PASSES)
         ]
         relu_h = [keep.tile([P, PACK, TOKENS], F32, name="relu_h%d" % c) for c in range(PASSES)]
         h_grouped = [keep.tile([P, TOKENS, PACK], BF16, name="h_grouped%d" % c, align_bytes=64) for c in range(PASSES)]
         h_codes = keep.tile([P, PASSES, TOKENS], U32, align_bytes=64)
         h_scales = keep.tile([P, PASSES, TOKENS], U8, align_bytes=64)
+        w2_grouped = [keep.tile([P, D, PACK], BF16, name="w2_grouped%d" % c, align_bytes=64) for c in range(PASSES)]
         w2_codes = keep.tile([P, PASSES, D], U32, align_bytes=64)
         w2_scales = keep.tile([P, PASSES, D], U8, align_bytes=64)
-        w2_grouped = [keep.tile([P, D, PACK], BF16, name="w2_grouped%d" % c, align_bytes=64) for c in range(PASSES)]
         out_ps = [psum.tile([P, E_HALF], F32, name="out_ps%d" % half) for half in range(HALVES)]
 
-        def regroup_w1(c):
-            source = w1_raw[c][:].rearrange("p l (j f t) -> p t l f j", j=PACK, t=PACK)
-            target = w1_grouped[c][:].rearrange("p t (l f) j -> p t l f j", l=PASS_LEAVES)
+        def regroup_w1(c, part):
+            leaves = slice(part * LOAD_LEAVES, (part + 1) * LOAD_LEAVES)
+            source = w1_raw[c][part][:].rearrange("p l (j f t) -> p t l f j", j=PACK, t=PACK)
+            target = w1_grouped[c][:].rearrange("p t (l f) j -> p t l f j", l=PASS_LEAVES)[:, :, leaves]
             nc.vector.tensor_copy(out=target[:, 0:T_HALF], in_=source[:, 0:T_HALF])
             for t in range(T_HALF, PACK):
                 nc.scalar.copy(out=target[:, t], in_=source[:, t])
@@ -152,11 +106,10 @@ def tile_fastfeedforwardnetwork_pa_s_kernel(tc, x, node_logits, node_b, w1, b1, 
                 scales=w1_scales[:, c, ts, :].rearrange("p t m -> p (t m)"),
                 in_=w1_grouped[c][:, ts].rearrange("p t m j -> p (t m j)"),
             )
-            pre_h = psum_h.tile([P, T_HALF, TOKENS], F32)
             for i in range(T_HALF):
                 t = half * T_HALF + i
                 nc.tensor.matmul_mx(
-                    out=pre_h[:, i, :],
+                    out=pre_h[c][half][:, i, :],
                     lhsT=w1_codes[:, c, t, :].bitcast(FP8X4),
                     lhsT_scale=w1_scales[:, c, t, :],
                     rhs=x_codes[:].bitcast(FP8X4),
@@ -164,10 +117,15 @@ def tile_fastfeedforwardnetwork_pa_s_kernel(tc, x, node_logits, node_b, w1, b1, 
                     start=True,
                     stop=True,
                 )
-            for i in range(T_HALF):
-                t = half * T_HALF + i
+
+        def bias_relu(c):
+            for t in range(PACK):
                 nc.scalar.activation(
-                    out=relu_h[c][:, t, :], in_=pre_h[:, i, :], func=ACT.Relu, bias=b1_cols[:, c, t : t + 1], scale=1.0
+                    out=relu_h[c][:, t, :],
+                    in_=pre_h[c][t // T_HALF][:, t % T_HALF, :],
+                    func=ACT.Relu,
+                    bias=b1_cols[:, c, t : t + 1],
+                    scale=1.0,
                 )
 
         def weight_hidden(c):
@@ -212,14 +170,60 @@ def tile_fastfeedforwardnetwork_pa_s_kernel(tc, x, node_logits, node_b, w1, b1, 
                 stop=(c == PASSES - 1),
             )
 
-        regroup_w1(0)
+        pre_gate = keep.tile([P, NODES], F32)
+        nc.vector.tensor_tensor(out=pre_gate[:], in0=logits[:], in1=node_bias[:], op=ALU.add)
+        gates = keep.tile([P, 2, NODES], F32)
+        nc.scalar.activation(out=gates[:, 0, :], in_=pre_gate[:], func=ACT.Sigmoid)
+        nc.scalar.activation(out=gates[:, 1, :], in_=pre_gate[:], func=ACT.Sigmoid, scale=-1.0)
+        upper = keep.tile([P, 2, 2], F32)
+        nc.vector.tensor_tensor(
+            out=upper[:],
+            in0=gates[:, :, 0].unsqueeze(2).to_broadcast([P, 2, 2]),
+            in1=gates[:, :, 1:3].rearrange("p s n -> p n s"),
+            op=ALU.mult,
+        )
+        lower = keep.tile([P, 4, 2, 2], F32)
+        nc.vector.tensor_tensor(
+            out=lower[:],
+            in0=gates[:, :, 3:7].rearrange("p s n -> p n s").unsqueeze(3).to_broadcast([P, 4, 2, 2]),
+            in1=gates[:, :, 7:15].rearrange("p s (n a) -> p n a s", a=2),
+            op=ALU.mult,
+        )
+
+        regroup_w1(0, 0)
+
+        leaf_probs = keep.tile([P, 4, 4, F_WORDS], F32)
+        nc.vector.tensor_tensor(
+            out=leaf_probs[:],
+            in0=upper[:].rearrange("p n s -> p (n s)").unsqueeze(2).unsqueeze(3).to_broadcast([P, 4, 4, F_WORDS]),
+            in1=lower[:].rearrange("p n a s -> p n (a s)").unsqueeze(3).to_broadcast([P, 4, 4, F_WORDS]),
+            op=ALU.mult,
+        )
+        leaf_cols = leaf_probs[:].rearrange("p u v r -> p (u v r)")
+
+        x_words = x_rows[:].bitcast(F32).rearrange("r (p u) -> r u p", u=2)
+        x_t = psum.tile([P, 2, TOKENS], F32)
+        for u in range(2):
+            nc.tensor.transpose(out=x_t[:, u, :], in_=x_words[:, u, :], identity=identity[:])
+        probs_t = psum.tile([P, PASSES, TOKENS], F32)
         for c in range(PASSES):
-            hidden_products(c, 0)
-            if c + 1 < PASSES:
-                regroup_w1(c + 1)
-            else:
+            nc.tensor.transpose(out=probs_t[:, c, :], in_=leaf_cols[:, c * P : (c + 1) * P], identity=identity[:])
+
+        nc.vector.tensor_copy(
+            out=x_grouped[:].bitcast(F32).rearrange("p (r u) -> p r u", u=2),
+            in_=x_t[:].rearrange("p u r -> p r u"),
+        )
+        regroup_w1(0, 1)
+        nc.vector.quantize_mx(out=x_codes[:].bitcast(FP8X4), scales=x_scales[:], in_=x_grouped[:])
+
+        for c in range(PASSES):
+            for half in range(HALVES):
+                hidden_products(c, half)
+                if c + 1 < PASSES:
+                    regroup_w1(c + 1, half)
+            if c + 1 == PASSES:
                 regroup_w2(0)
-            hidden_products(c, 1)
+            bias_relu(c)
 
         for c in range(PASSES):
             weight_hidden(c)

@@ -93,11 +93,12 @@ def tile_fastfeedforwardnetwork_pa_s_kernel(tc, x, node_logits, node_b, w1, b1, 
 
         def regroup_w1(c, part):
             leaves = slice(part * LOAD_LEAVES, (part + 1) * LOAD_LEAVES)
-            source = w1_raw[c][part][:].rearrange("p l (j f t) -> p t l f j", j=PACK, t=PACK)
-            target = w1_grouped[c][:].rearrange("p t (l f) j -> p t l f j", l=PASS_LEAVES)[:, :, leaves]
-            nc.vector.tensor_copy(out=target[:, 0:T_HALF], in_=source[:, 0:T_HALF])
-            for t in range(T_HALF, PACK):
-                nc.scalar.copy(out=target[:, t], in_=source[:, t])
+            source = w1_raw[c][part][:].rearrange("p l (j f t) -> p l f j t", j=PACK, t=PACK)
+            target = w1_grouped[c][:].rearrange("p t (l f) j -> p l f j t", l=PASS_LEAVES)[:, leaves]
+            vector_leaves = LOAD_LEAVES // HALVES
+            nc.vector.tensor_copy(out=target[:, 0:vector_leaves], in_=source[:, 0:vector_leaves])
+            for leaf in range(vector_leaves, LOAD_LEAVES):
+                nc.scalar.copy(out=target[:, leaf], in_=source[:, leaf])
 
         def hidden_products(c, half):
             ts = slice(half * T_HALF, (half + 1) * T_HALF)

@@ -68,7 +68,8 @@ def tile_fastfeedforwardnetwork_pa_s_kernel(tc, x, node_logits, node_b, w1, b1, 
         )
 
         identity = keep.tile([P, P], F32)
-        make_identity(nc, identity[:])
+        nc.vector.memset(identity[:], 0.0)
+        make_identity(nc, identity[:], nomemset=True)
 
         x_grouped = keep.tile([P, TOKENS * PACK], BF16, align_bytes=64)
         x_codes = keep.tile([P, TOKENS], U32, align_bytes=64)

@@ -40,32 +40,49 @@ def tile_fastfeedforwardnetwork_pa_s_kernel(tc, x, node_logits, node_b, w1, b1, 
         ctx.enter_context(tc.manual_schedule())
 
         logits = keep.tile([P, NODES], BF16)
-        nc.sync.dma_start(out=logits[:], in_=node_logits.flatten_outer_dims())
         node_bias = keep.tile([P, NODES], BF16)
-        nc.sync.dma_start(out=node_bias[:], in_=node_b.partition_broadcast(P))
         x_rows = keep.tile([P, D], BF16)
-        nc.sync.dma_start(out=x_rows[:], in_=x.flatten_outer_dims())
         w1_raw = [
             [keep.tile([P, LOAD_LEAVES, PACK * F], BF16, name="w1_raw%d_%d" % (c, part)) for part in range(HALVES)]
             for c in range(PASSES)
         ]
-        for c in range(PASSES):
-            for part in range(HALVES):
-                first = c * PASS_LEAVES + part * LOAD_LEAVES
-                nc.sync.dma_start(
-                    out=w1_raw[c][part][:],
-                    in_=w1[first : first + LOAD_LEAVES].rearrange("l (p j) f -> p l (j f)", j=PACK),
-                )
         w2_rows = w2.rearrange("l f e -> (l f) e")
         w2_raw = [keep.tile([P, PACK, D], BF16, name="w2_raw%d" % c) for c in range(PASSES)]
-        for c in range(PASSES):
+        b1_cols = keep.tile([P, PASSES, PACK], BF16)
+
+        def load_gates():
+            nc.sync.dma_start(out=logits[:], in_=node_logits.flatten_outer_dims())
+            nc.sync.dma_start(out=node_bias[:], in_=node_b.partition_broadcast(P))
+
+        def load_x():
+            nc.sync.dma_start(out=x_rows[:], in_=x.flatten_outer_dims())
+
+        def load_w1(c, part):
+            first = c * PASS_LEAVES + part * LOAD_LEAVES
+            nc.sync.dma_start(
+                out=w1_raw[c][part][:],
+                in_=w1[first : first + LOAD_LEAVES].rearrange("l (p j) f -> p l (j f)", j=PACK),
+            )
+
+        def load_w2(c):
             k_rows = slice(c * K_PASS, (c + 1) * K_PASS)
             nc.sync.dma_start(out=w2_raw[c][:], in_=w2_rows[k_rows].rearrange("(p t) e -> p t e", t=PACK))
-        b1_cols = keep.tile([P, PASSES, PACK], BF16)
-        nc.scalar.dma_start(
-            out=b1_cols[:],
-            in_=b1.rearrange("l f -> (l f)").rearrange("(c m t) -> m c t", c=PASSES, t=PACK),
-        )
+
+        def load_b1():
+            nc.scalar.dma_start(
+                out=b1_cols[:],
+                in_=b1.rearrange("l f -> (l f)").rearrange("(c m t) -> m c t", c=PASSES, t=PACK),
+            )
+
+        load_b1()
+        load_w1(0, 0)
+        load_gates()
+        load_x()
+        load_w1(0, 1)
+        for part in range(HALVES):
+            load_w1(1, part)
+        for c in range(PASSES):
+            load_w2(c)
 
         identity = keep.tile([P, P], F32)
         nc.vector.memset(identity[:], 0.0)
@@ -173,50 +190,71 @@ def tile_fastfeedforwardnetwork_pa_s_kernel(tc, x, node_logits, node_b, w1, b1, 
             )
 
         pre_gate = keep.tile([P, NODES], F32)
-        nc.vector.tensor_tensor(out=pre_gate[:], in0=logits[:], in1=node_bias[:], op=ALU.add)
         gates = keep.tile([P, 2, NODES], F32)
-        nc.scalar.activation(out=gates[:, 0, :], in_=pre_gate[:], func=ACT.Sigmoid)
-        nc.scalar.activation(out=gates[:, 1, :], in_=pre_gate[:], func=ACT.Sigmoid, scale=-1.0)
         upper = keep.tile([P, 2, 2], F32)
-        nc.vector.tensor_tensor(
-            out=upper[:],
-            in0=gates[:, :, 0].unsqueeze(2).to_broadcast([P, 2, 2]),
-            in1=gates[:, :, 1:3].rearrange("p s n -> p n s"),
-            op=ALU.mult,
-        )
         lower = keep.tile([P, 4, 2, 2], F32)
-        nc.vector.tensor_tensor(
-            out=lower[:],
-            in0=gates[:, :, 3:7].rearrange("p s n -> p n s").unsqueeze(3).to_broadcast([P, 4, 2, 2]),
-            in1=gates[:, :, 7:15].rearrange("p s (n a) -> p n a s", a=2),
-            op=ALU.mult,
-        )
-
-        regroup_w1(0, 0)
-
         leaf_probs = keep.tile([P, 4, 4, F_WORDS], F32)
-        nc.vector.tensor_tensor(
-            out=leaf_probs[:],
-            in0=upper[:].rearrange("p n s -> p (n s)").unsqueeze(2).unsqueeze(3).to_broadcast([P, 4, 4, F_WORDS]),
-            in1=lower[:].rearrange("p n a s -> p n (a s)").unsqueeze(3).to_broadcast([P, 4, 4, F_WORDS]),
-            op=ALU.mult,
-        )
         leaf_cols = leaf_probs[:].rearrange("p u v r -> p (u v r)")
-
         x_words = x_rows[:].bitcast(F32).rearrange("r (p u) -> r u p", u=2)
         x_t = psum.tile([P, 2, TOKENS], F32)
-        for u in range(2):
-            nc.tensor.transpose(out=x_t[:, u, :], in_=x_words[:, u, :], identity=identity[:])
         probs_t = psum.tile([P, PASSES, TOKENS], F32)
-        for c in range(PASSES):
-            nc.tensor.transpose(out=probs_t[:, c, :], in_=leaf_cols[:, c * P : (c + 1) * P], identity=identity[:])
 
-        nc.vector.tensor_copy(
-            out=x_grouped[:].bitcast(F32).rearrange("p (r u) -> p r u", u=2),
-            in_=x_t[:].rearrange("p u r -> p r u"),
-        )
+        def gate_sums():
+            nc.vector.tensor_tensor(out=pre_gate[:], in0=logits[:], in1=node_bias[:], op=ALU.add)
+
+        def gate_sigmoids():
+            nc.scalar.activation(out=gates[:, 0, :], in_=pre_gate[:], func=ACT.Sigmoid)
+            nc.scalar.activation(out=gates[:, 1, :], in_=pre_gate[:], func=ACT.Sigmoid, scale=-1.0)
+
+        def level_products():
+            nc.vector.tensor_tensor(
+                out=upper[:],
+                in0=gates[:, :, 0].unsqueeze(2).to_broadcast([P, 2, 2]),
+                in1=gates[:, :, 1:3].rearrange("p s n -> p n s"),
+                op=ALU.mult,
+            )
+            nc.vector.tensor_tensor(
+                out=lower[:],
+                in0=gates[:, :, 3:7].rearrange("p s n -> p n s").unsqueeze(3).to_broadcast([P, 4, 2, 2]),
+                in1=gates[:, :, 7:15].rearrange("p s (n a) -> p n a s", a=2),
+                op=ALU.mult,
+            )
+
+        def leaf_products():
+            nc.vector.tensor_tensor(
+                out=leaf_probs[:],
+                in0=upper[:].rearrange("p n s -> p (n s)").unsqueeze(2).unsqueeze(3).to_broadcast([P, 4, 4, F_WORDS]),
+                in1=lower[:].rearrange("p n a s -> p n (a s)").unsqueeze(3).to_broadcast([P, 4, 4, F_WORDS]),
+                op=ALU.mult,
+            )
+
+        def transpose_x():
+            for u in range(2):
+                nc.tensor.transpose(out=x_t[:, u, :], in_=x_words[:, u, :], identity=identity[:])
+
+        def transpose_probs():
+            for c in range(PASSES):
+                nc.tensor.transpose(out=probs_t[:, c, :], in_=leaf_cols[:, c * P : (c + 1) * P], identity=identity[:])
+
+        def group_x():
+            nc.vector.tensor_copy(
+                out=x_grouped[:].bitcast(F32).rearrange("p (r u) -> p r u", u=2),
+                in_=x_t[:].rearrange("p u r -> p r u"),
+            )
+
+        def quantise_x():
+            nc.vector.quantize_mx(out=x_codes[:].bitcast(FP8X4), scales=x_scales[:], in_=x_grouped[:])
+
+        regroup_w1(0, 0)
+        gate_sums()
+        gate_sigmoids()
+        transpose_x()
+        group_x()
+        level_products()
         regroup_w1(0, 1)
-        nc.vector.quantize_mx(out=x_codes[:].bitcast(FP8X4), scales=x_scales[:], in_=x_grouped[:])
+        leaf_products()
+        transpose_probs()
+        quantise_x()
 
         for c in range(PASSES):
             for half in range(HALVES):

@@ -245,6 +245,9 @@ def tile_fastfeedforwardnetwork_pa_s_kernel(tc, x, node_logits, node_b, w1, b1, 
         def quantise_x():
             nc.vector.quantize_mx(out=x_codes[:].bitcast(FP8X4), scales=x_scales[:], in_=x_grouped[:])
 
+        warm = keep.tile([P, 1], F32)
+        nc.vector.memset(warm[:], 0.0)
+        nc.scalar.activation(out=warm[:], in_=warm[:], func=ACT.Sigmoid)
         regroup_w1(0, 0)
         gate_sums()
         gate_sigmoids()

@@ -22,9 +22,12 @@ NODES = LEAVES - 1
 F = 64
 PASSES = LEAVES * F // K_PASS
 PASS_LEAVES = LEAVES // PASSES
-F_WORDS = F // PACK
+PAIR = 2
+CHUNKS = 4
+F_PAIRS = F // PAIR
 HALVES = 2
 E_HALF = D // HALVES
+PIECES = ((0, 256), (256, 384), (384, 512))
 T_HALF = PACK // HALVES
 LOAD_LEAVES = PASS_LEAVES // HALVES
 
@@ -48,7 +51,7 @@ def tile_fastfeedforwardnetwork_pa_s_kernel(tc, x, node_logits, node_b, w1, b1, 
         ]
         w2_rows = w2.rearrange("l f e -> (l f) e")
         w2_raw = [keep.tile([P, PACK, D], BF16, name="w2_raw%d" % c) for c in range(PASSES)]
-        b1_cols = keep.tile([P, PASSES, PACK], BF16)
+        b1_cols = keep.tile([P, CHUNKS, PAIR], BF16)
 
         def load_gates():
             nc.sync.dma_start(out=logits[:], in_=node_logits.flatten_outer_dims())
@@ -66,12 +69,12 @@ def tile_fastfeedforwardnetwork_pa_s_kernel(tc, x, node_logits, node_b, w1, b1, 
 
         def load_w2(c):
             k_rows = slice(c * K_PASS, (c + 1) * K_PASS)
-            nc.sync.dma_start(out=w2_raw[c][:], in_=w2_rows[k_rows].rearrange("(p t) e -> p t e", t=PACK))
+            nc.sync.dma_start(out=w2_raw[c][:].rearrange("p (u e) n -> p u (e n)", u=HALVES), in_=w2_rows[k_rows].rearrange("(u p e) n -> p u (e n)", u=HALVES, e=PAIR))
 
         def load_b1():
             nc.scalar.dma_start(
                 out=b1_cols[:],
-                in_=b1.rearrange("l f -> (l f)").rearrange("(c m t) -> m c t", c=PASSES, t=PACK),
+                in_=b1.rearrange("l f -> (l f)").rearrange("(cu m e) -> m cu e", cu=CHUNKS, e=PAIR),
             )
 
         load_b1()
@@ -92,7 +95,8 @@ def tile_fastfeedforwardnetwork_pa_s_kernel(tc, x, node_logits, node_b, w1, b1, 
         x_codes = keep.tile([P, TOKENS], U32, align_bytes=64)
         x_scales = keep.tile([P, TOKENS], U8, align_bytes=64)
         w1_grouped = [
-            keep.tile([P, PACK, P, PACK], BF16, name="w1_grouped%d" % c, align_bytes=64) for c in range(PASSES)
+            [keep.tile([P, PAIR, P, PACK], BF16, name="w1_grouped%d_%d" % (c, u), align_bytes=64) for u in range(HALVES)]
+            for c in range(PASSES)
         ]
         w1_codes = keep.tile([P, PASSES, PACK, P], U32, align_bytes=64)
         w1_scales = keep.tile([P, PASSES, PACK, P], U8, align_bytes=64)
@@ -107,28 +111,27 @@ def tile_fastfeedforwardnetwork_pa_s_kernel(tc, x, node_logits, node_b, w1, b1, 
         w2_grouped = [keep.tile([P, D, PACK], BF16, name="w2_grouped%d" % c, align_bytes=64) for c in range(PASSES)]
         w2_codes = keep.tile([P, PASSES, D], U32, align_bytes=64)
         w2_scales = keep.tile([P, PASSES, D], U8, align_bytes=64)
-        out_ps = [psum.tile([P, E_HALF], F32, name="out_ps%d" % half) for half in range(HALVES)]
 
-        def regroup_w1(c, part):
-            leaves = slice(part * LOAD_LEAVES, (part + 1) * LOAD_LEAVES)
-            source = w1_raw[c][part][:].rearrange("p l (j f t) -> p l f j t", j=PACK, t=PACK)
-            target = w1_grouped[c][:].rearrange("p t (l f) j -> p l f j t", l=PASS_LEAVES)[:, leaves]
+        def regroup_w1(c, u):
+            source = w1_raw[c][u][:].rearrange("p l (j i e) -> p l i j e", j=PACK, e=PAIR)
+            target = w1_grouped[c][u][:].rearrange("p e (l i) j -> p l i j e", l=LOAD_LEAVES)
             vector_leaves = LOAD_LEAVES // HALVES
             nc.vector.tensor_copy(out=target[:, 0:vector_leaves], in_=source[:, 0:vector_leaves])
-            for leaf in range(vector_leaves, LOAD_LEAVES):
-                nc.scalar.copy(out=target[:, leaf], in_=source[:, leaf])
+            nc.scalar.copy(out=target[:, vector_leaves:], in_=source[:, vector_leaves:])
 
-        def hidden_products(c, half):
-            ts = slice(half * T_HALF, (half + 1) * T_HALF)
+        def quantise_w1(c, u):
+            ts = slice(u * PAIR, (u + 1) * PAIR)
             nc.vector.quantize_mx(
                 out=w1_codes[:, c, ts, :].rearrange("p t m -> p (t m)").bitcast(FP8X4),
                 scales=w1_scales[:, c, ts, :].rearrange("p t m -> p (t m)"),
-                in_=w1_grouped[c][:, ts].rearrange("p t m j -> p (t m j)"),
+                in_=w1_grouped[c][u][:].rearrange("p e m j -> p (e m j)"),
             )
-            for i in range(T_HALF):
-                t = half * T_HALF + i
+
+        def hidden_products(c, u):
+            for e in range(PAIR):
+                t = PAIR * u + e
                 nc.tensor.matmul_mx(
-                    out=pre_h[c][half][:, i, :],
+                    out=pre_h[c][u][:, e, :],
                     lhsT=w1_codes[:, c, t, :].bitcast(FP8X4),
                     lhsT_scale=w1_scales[:, c, t, :],
                     rhs=x_codes[:].bitcast(FP8X4),
@@ -137,21 +140,24 @@ def tile_fastfeedforwardnetwork_pa_s_kernel(tc, x, node_logits, node_b, w1, b1, 
                     stop=True,
                 )
 
-        def bias_relu(c):
-            for t in range(PACK):
+        def bias_relu(c, u):
+            for e in range(PAIR):
                 nc.scalar.activation(
-                    out=relu_h[c][:, t, :],
-                    in_=pre_h[c][t // T_HALF][:, t % T_HALF, :],
+                    out=relu_h[c][:, PAIR * u + e, :],
+                    in_=pre_h[c][u][:, e, :],
                     func=ACT.Relu,
-                    bias=b1_cols[:, c, t : t + 1],
+                    bias=b1_cols[:, HALVES * c + u, e : e + 1],
                     scale=1.0,
                 )
 
         def weight_hidden(c):
             nc.vector.tensor_tensor(
-                out=h_grouped[c][:],
-                in0=relu_h[c][:].rearrange("p t r -> p r t"),
-                in1=probs_t[:, c, :].unsqueeze(2).to_broadcast([P, TOKENS, PACK]),
+                out=h_grouped[c][:].rearrange("p r (u e) -> p r u e", u=HALVES),
+                in0=relu_h[c][:].rearrange("p (u e) r -> p r u e", u=HALVES),
+                in1=probs_t[:, HALVES * c : HALVES * (c + 1), :]
+                .rearrange("p u r -> p r u")
+                .unsqueeze(3)
+                .to_broadcast([P, TOKENS, HALVES, PAIR]),
                 op=ALU.mult,
             )
 
@@ -169,18 +175,18 @@ def tile_fastfeedforwardnetwork_pa_s_kernel(tc, x, node_logits, node_b, w1, b1, 
             nc.vector.tensor_copy(out=target[:, 0:groups], in_=source[:, 0:groups])
             nc.scalar.copy(out=target[:, groups : 2 * groups], in_=source[:, groups : 2 * groups])
 
-        def quantise_w2(c, half):
-            e_cols = slice(half * E_HALF, (half + 1) * E_HALF)
+        def quantise_w2(c, piece):
+            e_cols = slice(*PIECES[piece])
             nc.vector.quantize_mx(
                 out=w2_codes[:, c, e_cols].bitcast(FP8X4),
                 scales=w2_scales[:, c, e_cols],
                 in_=w2_grouped[c][:, e_cols, :].rearrange("p e t -> p (e t)"),
             )
 
-        def output_product(c, half):
-            e_cols = slice(half * E_HALF, (half + 1) * E_HALF)
+        def output_product(c, piece):
+            e_cols = slice(*PIECES[piece])
             nc.tensor.matmul_mx(
-                out=out_ps[half][:],
+                out=out_ps[piece][:],
                 lhsT=h_codes[:, c, :].bitcast(FP8X4),
                 lhsT_scale=h_scales[:, c, :],
                 rhs=w2_codes[:, c, e_cols].bitcast(FP8X4),
@@ -193,11 +199,11 @@ def tile_fastfeedforwardnetwork_pa_s_kernel(tc, x, node_logits, node_b, w1, b1, 
         gates = keep.tile([P, 2, NODES], F32)
         upper = keep.tile([P, 2, 2], F32)
         lower = keep.tile([P, 4, 2, 2], F32)
-        leaf_probs = keep.tile([P, 4, 4, F_WORDS], F32)
+        leaf_probs = keep.tile([P, 4, 4, F_PAIRS], F32)
         leaf_cols = leaf_probs[:].rearrange("p u v r -> p (u v r)")
         x_words = x_rows[:].bitcast(F32).rearrange("r (p u) -> r u p", u=2)
-        x_t = psum.tile([P, 2, TOKENS], F32)
-        probs_t = psum.tile([P, PASSES, TOKENS], F32)
+        x_t = psum.tile([P, 2, TOKENS], F32, tag="x_bank", name="x_t")
+        probs_t = psum.tile([P, CHUNKS, TOKENS], F32)
 
         def gate_sums():
             nc.vector.tensor_tensor(out=pre_gate[:], in0=logits[:], in1=node_bias[:], op=ALU.add)
@@ -223,8 +229,8 @@ def tile_fastfeedforwardnetwork_pa_s_kernel(tc, x, node_logits, node_b, w1, b1, 
         def leaf_products():
             nc.vector.tensor_tensor(
                 out=leaf_probs[:],
-                in0=upper[:].rearrange("p n s -> p (n s)").unsqueeze(2).unsqueeze(3).to_broadcast([P, 4, 4, F_WORDS]),
-                in1=lower[:].rearrange("p n a s -> p n (a s)").unsqueeze(3).to_broadcast([P, 4, 4, F_WORDS]),
+                in0=upper[:].rearrange("p n s -> p (n s)").unsqueeze(2).unsqueeze(3).to_broadcast([P, 4, 4, F_PAIRS]),
+                in1=lower[:].rearrange("p n a s -> p n (a s)").unsqueeze(3).to_broadcast([P, 4, 4, F_PAIRS]),
                 op=ALU.mult,
             )
 
@@ -233,8 +239,10 @@ def tile_fastfeedforwardnetwork_pa_s_kernel(tc, x, node_logits, node_b, w1, b1, 
                 nc.tensor.transpose(out=x_t[:, u, :], in_=x_words[:, u, :], identity=identity[:])
 
         def transpose_probs():
-            for c in range(PASSES):
-                nc.tensor.transpose(out=probs_t[:, c, :], in_=leaf_cols[:, c * P : (c + 1) * P], identity=identity[:])
+            for chunk in range(CHUNKS):
+                nc.tensor.transpose(
+                    out=probs_t[:, chunk, :], in_=leaf_cols[:, chunk * P : (chunk + 1) * P], identity=identity[:]
+                )
 
         def group_x():
             nc.vector.tensor_copy(
@@ -252,36 +260,52 @@ def tile_fastfeedforwardnetwork_pa_s_kernel(tc, x, node_logits, node_b, w1, b1, 
         gate_sums()
         gate_sigmoids()
         transpose_x()
+        quantise_w1(0, 0)
         group_x()
         level_products()
         regroup_w1(0, 1)
+        quantise_x()
+        hidden_products(0, 0)
+        quantise_w1(0, 1)
+        hidden_products(0, 1)
+        regroup_w1(1, 0)
         leaf_products()
         transpose_probs()
-        quantise_x()
+        bias_relu(0, 0)
+        regroup_w1(1, 1)
+        bias_relu(0, 1)
+        for u in range(HALVES):
+            quantise_w1(1, u)
+            hidden_products(1, u)
+        regroup_w2(0)
+        weight_hidden(0)
+        for u in range(HALVES):
+            bias_relu(1, u)
+        regroup_w2(1)
 
-        for c in range(PASSES):
-            for half in range(HALVES):
-                hidden_products(c, half)
-                if c + 1 < PASSES:
-                    regroup_w1(c + 1, half)
-            if c + 1 == PASSES:
-                regroup_w2(0)
-            bias_relu(c)
-
-        for c in range(PASSES):
-            weight_hidden(c)
-            quantise_w2(c, 0)
-            quantise_hidden(c)
-            output_product(c, 0)
-            if c + 1 < PASSES:
-                regroup_w2(c + 1)
-            quantise_w2(c, 1)
-            output_product(c, 1)
+        banks = ("out_bank0", "out_bank1", "x_bank")
+        out_ps = [
+            psum.tile([P, stop - first], F32, tag=bank, name="out_ps_%s" % bank)
+            for (first, stop), bank in zip(PIECES, banks)
+        ]
+        quantise_w2(0, 0)
+        quantise_hidden(0)
+        output_product(0, 0)
+        for piece in (1, 2):
+            quantise_w2(0, piece)
+            output_product(0, piece)
+        weight_hidden(1)
+        quantise_w2(1, 0)
+        quantise_hidden(1)
+        output_product(1, 0)
+        for piece in (1, 2):
+            quantise_w2(1, piece)
+            output_product(1, piece)
 
         out_rows = out.flatten_outer_dims()
-        result0 = keep.tile([P, E_HALF], F32)
-        nc.vector.tensor_copy(out=result0[:], in_=out_ps[0][:])
-        nc.sync.dma_start(out=out_rows[:, 0:E_HALF], in_=result0[:])
-        result1 = keep.tile([P, E_HALF], F32)
-        nc.scalar.copy(out=result1[:], in_=out_ps[1][:])
-        nc.sync.dma_start(out=out_rows[:, E_HALF:D], in_=result1[:])
+        result = [keep.tile([P, stop - first], F32, name="result%d" % first) for first, stop in PIECES]
+        nc.scalar.copy(out=result[0][:], in_=out_ps[0][:])
+        for piece in (1, 2):
+            nc.vector.tensor_copy(out=result[piece][:], in_=out_ps[piece][:])
+        for piece, (first, stop) in enumerate(PIECES):
+            nc.sync.dma_start(out=out_rows[:, first:stop], in_=result[piece][:])

@@ -51,7 +51,7 @@ def tile_fastfeedforwardnetwork_pa_s_kernel(tc, x, node_logits, node_b, w1, b1, 
         ]
         w2_rows = w2.rearrange("l f e -> (l f) e")
         w2_raw = [keep.tile([P, PACK, D], BF16, name="w2_raw%d" % c) for c in range(PASSES)]
-        b1_cols = keep.tile([P, CHUNKS, PAIR], BF16)
+        b1_rows = keep.tile([P, P * PAIR], BF16)
 
         def load_gates():
             nc.sync.dma_start(out=logits[:], in_=node_logits.flatten_outer_dims())
@@ -72,9 +72,10 @@ def tile_fastfeedforwardnetwork_pa_s_kernel(tc, x, node_logits, node_b, w1, b1, 
             nc.sync.dma_start(out=w2_raw[c][:].rearrange("p (u e) n -> p u (e n)", u=HALVES), in_=w2_rows[k_rows].rearrange("(u p e) n -> p u (e n)", u=HALVES, e=PAIR))
 
         def load_b1():
+            nc.vector.memset(b1_rows[:], 0.0)
             nc.scalar.dma_start(
-                out=b1_cols[:],
-                in_=b1.rearrange("l f -> (l f)").rearrange("(cu m e) -> m cu e", cu=CHUNKS, e=PAIR),
+                out=b1_rows[0:CHUNKS, :],
+                in_=b1.rearrange("l f -> (l f)").rearrange("(q n) -> q n", q=CHUNKS),
             )
 
         load_b1()
@@ -203,6 +204,8 @@ def tile_fastfeedforwardnetwork_pa_s_kernel(tc, x, node_logits, node_b, w1, b1, 
         leaf_cols = leaf_probs[:].rearrange("p u v r -> p (u v r)")
         x_words = x_rows[:].bitcast(F32).rearrange("r (p u) -> r u p", u=2)
         x_t = psum.tile([P, 2, TOKENS], F32, tag="x_bank", name="x_t")
+        b1_t = psum.tile([P, P], F32, tag="out_bank1", name="b1_t")
+        b1_cols = keep.tile([P, CHUNKS, PAIR], BF16)
         probs_t = psum.tile([P, CHUNKS, TOKENS], F32)
 
         def gate_sums():
@@ -238,6 +241,10 @@ def tile_fastfeedforwardnetwork_pa_s_kernel(tc, x, node_logits, node_b, w1, b1, 
             for u in range(2):
                 nc.tensor.transpose(out=x_t[:, u, :], in_=x_words[:, u, :], identity=identity[:])
 
+        def transpose_b1():
+            nc.tensor.transpose(out=b1_t[:], in_=b1_rows[:].bitcast(F32), identity=identity[:])
+            nc.scalar.copy(out=b1_cols[:].rearrange("p q e -> p (q e)").bitcast(F32), in_=b1_t[:, 0:CHUNKS])
+
         def transpose_probs():
             for chunk in range(CHUNKS):
                 nc.tensor.transpose(
@@ -258,6 +265,7 @@ def tile_fastfeedforwardnetwork_pa_s_kernel(tc, x, node_logits, node_b, w1, b1, 
         nc.scalar.activation(out=warm[:], in_=warm[:], func=ACT.Sigmoid)
         regroup_w1(0, 0)
         gate_sums()
+        transpose_b1()
         gate_sigmoids()
         transpose_x()
         quantise_w1(0, 0)

@@ -80,8 +80,8 @@ def tile_fastfeedforwardnetwork_pa_s_kernel(tc, x, node_logits, node_b, w1, b1, 
 
         load_b1()
         load_w1(0, 0)
-        load_gates()
         load_x()
+        load_gates()
         load_w1(0, 1)
         for part in range(HALVES):
             load_w1(1, part)
@@ -230,12 +230,14 @@ def tile_fastfeedforwardnetwork_pa_s_kernel(tc, x, node_logits, node_b, w1, b1, 
             )
 
         def leaf_products():
-            nc.vector.tensor_tensor(
-                out=leaf_probs[:],
-                in0=upper[:].rearrange("p n s -> p (n s)").unsqueeze(2).unsqueeze(3).to_broadcast([P, 4, 4, F_PAIRS]),
-                in1=lower[:].rearrange("p n a s -> p n (a s)").unsqueeze(3).to_broadcast([P, 4, 4, F_PAIRS]),
-                op=ALU.mult,
-            )
+            for q in range(CHUNKS):
+                nc.vector.tensor_scalar(
+                    out=leaf_probs[:, q],
+                    in0=lower[:, q].rearrange("p a s -> p (a s)").unsqueeze(2).to_broadcast([P, 4, F_PAIRS]),
+                    scalar1=upper[:].rearrange("p n s -> p (n s)")[:, q : q + 1],
+                    scalar2=None,
+                    op0=ALU.mult,
+                )
 
         def transpose_x():
             for u in range(2):
@@ -243,6 +245,8 @@ def tile_fastfeedforwardnetwork_pa_s_kernel(tc, x, node_logits, node_b, w1, b1, 
 
         def transpose_b1():
             nc.tensor.transpose(out=b1_t[:], in_=b1_rows[:].bitcast(F32), identity=identity[:])
+
+        def keep_b1():
             nc.scalar.copy(out=b1_cols[:].rearrange("p q e -> p (q e)").bitcast(F32), in_=b1_t[:, 0:CHUNKS])
 
         def transpose_probs():
@@ -265,13 +269,14 @@ def tile_fastfeedforwardnetwork_pa_s_kernel(tc, x, node_logits, node_b, w1, b1, 
         nc.scalar.activation(out=warm[:], in_=warm[:], func=ACT.Sigmoid)
         regroup_w1(0, 0)
         gate_sums()
-        transpose_b1()
         gate_sigmoids()
         transpose_x()
+        transpose_b1()
         quantise_w1(0, 0)
         group_x()
         level_products()
         regroup_w1(0, 1)
+        keep_b1()
         quantise_x()
         hidden_products(0, 0)
         quantise_w1(0, 1)

@@ -23,6 +23,7 @@ F = 64
 PASSES = LEAVES * F // K_PASS
 PASS_LEAVES = LEAVES // PASSES
 PAIR = 2
+RUN = 4
 CHUNKS = 4
 F_PAIRS = F // PAIR
 HALVES = 2
@@ -43,7 +44,10 @@ def tile_fastfeedforwardnetwork_pa_s_kernel(tc, x, node_logits, node_b, w1, b1, 
         ctx.enter_context(tc.manual_schedule())
 
         logits = keep.tile([P, NODES], BF16)
-        node_bias = keep.tile([P, NODES], BF16)
+        bias_row = keep.tile([P, NODES + 1], BF16)
+        nc.vector.memset(bias_row[:], 0.0)
+        ones = keep.tile([P, P], BF16)
+        nc.vector.memset(ones[:], 1.0)
         x_rows = keep.tile([P, D], BF16)
         w1_raw = [
             [keep.tile([P, LOAD_LEAVES, PACK * F], BF16, name="w1_raw%d_%d" % (c, part)) for part in range(HALVES)]
@@ -55,7 +59,7 @@ def tile_fastfeedforwardnetwork_pa_s_kernel(tc, x, node_logits, node_b, w1, b1, 
 
         def load_gates():
             nc.sync.dma_start(out=logits[:], in_=node_logits.flatten_outer_dims())
-            nc.sync.dma_start(out=node_bias[:], in_=node_b.partition_broadcast(P))
+            nc.sync.dma_start(out=bias_row[0:1, 0:NODES], in_=node_b.unsqueeze(0))
 
         def load_x():
             nc.sync.dma_start(out=x_rows[:], in_=x.flatten_outer_dims())
@@ -203,13 +207,18 @@ def tile_fastfeedforwardnetwork_pa_s_kernel(tc, x, node_logits, node_b, w1, b1, 
         leaf_probs = keep.tile([P, 4, 4, F_PAIRS], F32)
         leaf_cols = leaf_probs[:].rearrange("p u v r -> p (u v r)")
         x_words = x_rows[:].bitcast(F32).rearrange("r (p u) -> r u p", u=2)
-        x_t = psum.tile([P, 2, TOKENS], F32, tag="x_bank", name="x_t")
+        x_bank = psum.tile([P, 2 * TOKENS + NODES + 1], F32, tag="x_bank", name="x_bank")
+        x_t = x_bank[:, 0 : 2 * TOKENS].rearrange("p (u r) -> p u r", u=2)
+        node_bias = x_bank[:, 2 * TOKENS : 2 * TOKENS + NODES]
         b1_t = psum.tile([P, P], F32, tag="out_bank1", name="b1_t")
         b1_cols = keep.tile([P, CHUNKS, PAIR], BF16)
         probs_t = psum.tile([P, CHUNKS, TOKENS], F32)
 
+        def spread_node_bias():
+            nc.tensor.matmul(out=node_bias, lhsT=ones[:], rhs=bias_row[:, 0:NODES], start=True, stop=True)
+
         def gate_sums():
-            nc.vector.tensor_tensor(out=pre_gate[:], in0=logits[:], in1=node_bias[:], op=ALU.add)
+            nc.vector.tensor_tensor(out=pre_gate[:], in0=logits[:], in1=node_bias, op=ALU.add)
 
         def gate_sigmoids():
             nc.scalar.activation(out=gates[:, 0, :], in_=pre_gate[:], func=ACT.Sigmoid)
@@ -257,8 +266,8 @@ def tile_fastfeedforwardnetwork_pa_s_kernel(tc, x, node_logits, node_b, w1, b1, 
 
         def group_x():
             nc.vector.tensor_copy(
-                out=x_grouped[:].bitcast(F32).rearrange("p (r u) -> p r u", u=2),
-                in_=x_t[:].rearrange("p u r -> p r u"),
+                out=x_grouped[:].bitcast(F32).rearrange("p (g i u) -> p g u i", i=RUN, u=2),
+                in_=x_t.rearrange("p u (g i) -> p g u i", i=RUN),
             )
 
         def quantise_x():
@@ -268,19 +277,20 @@ def tile_fastfeedforwardnetwork_pa_s_kernel(tc, x, node_logits, node_b, w1, b1, 
         nc.vector.memset(warm[:], 0.0)
         nc.scalar.activation(out=warm[:], in_=warm[:], func=ACT.Sigmoid)
         regroup_w1(0, 0)
-        gate_sums()
-        gate_sigmoids()
         transpose_x()
+        spread_node_bias()
         transpose_b1()
         quantise_w1(0, 0)
         group_x()
-        level_products()
+        gate_sums()
         regroup_w1(0, 1)
+        gate_sigmoids()
         keep_b1()
         quantise_x()
         hidden_products(0, 0)
         quantise_w1(0, 1)
         hidden_products(0, 1)
+        level_products()
         regroup_w1(1, 0)
         leaf_products()
         transpose_probs()

@@ -23,6 +23,8 @@ F = 64
 PASSES = LEAVES * F // K_PASS
 PASS_LEAVES = LEAVES // PASSES
 PAIR = 2
+TOKEN_RUN = 4
+BIAS_COL = 64
 RUN = 4
 CHUNKS = 4
 F_PAIRS = F // PAIR
@@ -43,11 +45,8 @@ def tile_fastfeedforwardnetwork_pa_s_kernel(tc, x, node_logits, node_b, w1, b1, 
         psum = ctx.enter_context(tc.psum_pool(name="psum", bufs=1))
         ctx.enter_context(tc.manual_schedule())
 
-        logits = keep.tile([P, NODES], BF16)
-        bias_row = keep.tile([P, NODES + 1], BF16)
-        nc.vector.memset(bias_row[:], 0.0)
-        ones = keep.tile([P, P], BF16)
-        nc.vector.memset(ones[:], 1.0)
+        gate_rows = keep.tile([P, BIAS_COL + NODES + 1], BF16)
+        nc.vector.memset(gate_rows[:], 0.0)
         x_rows = keep.tile([P, D], BF16)
         w1_raw = [
             [keep.tile([P, LOAD_LEAVES, PACK * F], BF16, name="w1_raw%d_%d" % (c, part)) for part in range(HALVES)]
@@ -58,8 +57,11 @@ def tile_fastfeedforwardnetwork_pa_s_kernel(tc, x, node_logits, node_b, w1, b1, 
         b1_rows = keep.tile([P, P * PAIR], BF16)
 
         def load_gates():
-            nc.sync.dma_start(out=logits[:], in_=node_logits.flatten_outer_dims())
-            nc.sync.dma_start(out=bias_row[0:1, 0:NODES], in_=node_b.unsqueeze(0))
+            nc.sync.dma_start(out=gate_rows[0:1, BIAS_COL : BIAS_COL + NODES], in_=node_b.unsqueeze(0))
+            nc.sync.dma_start(
+                out=gate_rows[0 : TOKENS // TOKEN_RUN, 0 : TOKEN_RUN * NODES],
+                in_=node_logits.rearrange("b t n -> (b t n)").rearrange("(q s) -> q s", s=TOKEN_RUN * NODES),
+            )
 
         def load_x():
             nc.sync.dma_start(out=x_rows[:], in_=x.flatten_outer_dims())
@@ -95,6 +97,19 @@ def tile_fastfeedforwardnetwork_pa_s_kernel(tc, x, node_logits, node_b, w1, b1, 
         identity = keep.tile([P, P], F32)
         nc.vector.memset(identity[:], 0.0)
         make_identity(nc, identity[:], nomemset=True)
+        spread = keep.tile([P, TOKEN_RUN, TOKENS], BF16)
+        nc.vector.memset(spread[:], 0.0)
+        nc.gpsimd.affine_select(
+            out=spread[:],
+            in_=spread[:],
+            compare_op=ALU.not_equal,
+            fill=1.0,
+            base=0,
+            pattern=[[-1, TOKEN_RUN], [1, TOKENS]],
+            channel_multiplier=-TOKEN_RUN,
+        )
+        ones = keep.tile([P, P], BF16)
+        nc.vector.memset(ones[:], 1.0)
 
         x_grouped = keep.tile([P, TOKENS * PACK], BF16, align_bytes=64)
         x_codes = keep.tile([P, TOKENS], U32, align_bytes=64)
@@ -200,29 +215,35 @@ def tile_fastfeedforwardnetwork_pa_s_kernel(tc, x, node_logits, node_b, w1, b1, 
                 stop=(c == PASSES - 1),
             )
 
-        pre_gate = keep.tile([P, NODES], F32)
         gates = keep.tile([P, 2, NODES], F32)
         upper = keep.tile([P, 2, 2], F32)
         lower = keep.tile([P, 4, 2, 2], F32)
         leaf_probs = keep.tile([P, 4, 4, F_PAIRS], F32)
         leaf_cols = leaf_probs[:].rearrange("p u v r -> p (u v r)")
         x_words = x_rows[:].bitcast(F32).rearrange("r (p u) -> r u p", u=2)
-        x_bank = psum.tile([P, 2 * TOKENS + NODES + 1], F32, tag="x_bank", name="x_bank")
-        x_t = x_bank[:, 0 : 2 * TOKENS].rearrange("p (u r) -> p u r", u=2)
-        node_bias = x_bank[:, 2 * TOKENS : 2 * TOKENS + NODES]
-        b1_t = psum.tile([P, P], F32, tag="out_bank1", name="b1_t")
+        x_t = psum.tile([P, 2, TOKENS], F32, tag="x_bank", name="x_t")
+        small_t = psum.tile([P, P + NODES + 1], F32, tag="out_bank1", name="small_t")
+        b1_t = small_t[:, 0:P]
+        pre_gate = small_t[:, P : P + NODES]
         b1_cols = keep.tile([P, CHUNKS, PAIR], BF16)
         probs_t = psum.tile([P, CHUNKS, TOKENS], F32)
 
-        def spread_node_bias():
-            nc.tensor.matmul(out=node_bias, lhsT=ones[:], rhs=bias_row[:, 0:NODES], start=True, stop=True)
-
         def gate_sums():
-            nc.vector.tensor_tensor(out=pre_gate[:], in0=logits[:], in1=node_bias, op=ALU.add)
+            for i in range(TOKEN_RUN):
+                nc.tensor.matmul(
+                    out=pre_gate,
+                    lhsT=spread[:, i, :],
+                    rhs=gate_rows[:, i * NODES : (i + 1) * NODES],
+                    start=(i == 0),
+                    stop=False,
+                )
+            nc.tensor.matmul(
+                out=pre_gate, lhsT=ones[:], rhs=gate_rows[:, BIAS_COL : BIAS_COL + NODES], start=False, stop=True
+            )
 
         def gate_sigmoids():
-            nc.scalar.activation(out=gates[:, 0, :], in_=pre_gate[:], func=ACT.Sigmoid)
-            nc.scalar.activation(out=gates[:, 1, :], in_=pre_gate[:], func=ACT.Sigmoid, scale=-1.0)
+            nc.scalar.activation(out=gates[:, 0, :], in_=pre_gate, func=ACT.Sigmoid)
+            nc.scalar.activation(out=gates[:, 1, :], in_=pre_gate, func=ACT.Sigmoid, scale=-1.0)
 
         def level_products():
             nc.vector.tensor_tensor(
@@ -253,7 +274,7 @@ def tile_fastfeedforwardnetwork_pa_s_kernel(tc, x, node_logits, node_b, w1, b1, 
                 nc.tensor.transpose(out=x_t[:, u, :], in_=x_words[:, u, :], identity=identity[:])
 
         def transpose_b1():
-            nc.tensor.transpose(out=b1_t[:], in_=b1_rows[:].bitcast(F32), identity=identity[:])
+            nc.tensor.transpose(out=b1_t, in_=b1_rows[:].bitcast(F32), identity=identity[:])
 
         def keep_b1():
             nc.scalar.copy(out=b1_cols[:].rearrange("p q e -> p (q e)").bitcast(F32), in_=b1_t[:, 0:CHUNKS])
@@ -267,7 +288,7 @@ def tile_fastfeedforwardnetwork_pa_s_kernel(tc, x, node_logits, node_b, w1, b1, 
         def group_x():
             nc.vector.tensor_copy(
                 out=x_grouped[:].bitcast(F32).rearrange("p (g i u) -> p g u i", i=RUN, u=2),
-                in_=x_t.rearrange("p u (g i) -> p g u i", i=RUN),
+                in_=x_t[:].rearrange("p u (g i) -> p g u i", i=RUN),
             )
 
         def quantise_x():
@@ -278,11 +299,10 @@ def tile_fastfeedforwardnetwork_pa_s_kernel(tc, x, node_logits, node_b, w1, b1, 
         nc.scalar.activation(out=warm[:], in_=warm[:], func=ACT.Sigmoid)
         regroup_w1(0, 0)
         transpose_x()
-        spread_node_bias()
         transpose_b1()
+        gate_sums()
         quantise_w1(0, 0)
         group_x()
-        gate_sums()
         regroup_w1(0, 1)
         gate_sigmoids()
         keep_b1()
@@ -327,8 +347,8 @@ def tile_fastfeedforwardnetwork_pa_s_kernel(tc, x, node_logits, node_b, w1, b1, 
 
         out_rows = out.flatten_outer_dims()
         result = [keep.tile([P, stop - first], F32, name="result%d" % first) for first, stop in PIECES]
-        nc.scalar.copy(out=result[0][:], in_=out_ps[0][:])
-        for piece in (1, 2):
-            nc.vector.tensor_copy(out=result[piece][:], in_=out_ps[piece][:])
+        nc.vector.tensor_copy(out=result[0][:], in_=out_ps[0][:])
+        nc.scalar.copy(out=result[1][:], in_=out_ps[1][:])
+        nc.vector.tensor_copy(out=result[2][:], in_=out_ps[2][:])
         for piece, (first, stop) in enumerate(PIECES):
             nc.sync.dma_start(out=out_rows[:, first:stop], in_=result[piece][:])

from contextlib import ExitStack

import concourse.mybir as mybir
from concourse.masks import make_identity

BF16 = mybir.dt.bfloat16
F32 = mybir.dt.float32
U32 = mybir.dt.uint32
U8 = mybir.dt.uint8
FP8X4 = mybir.dt.float8_e4m3fn_x4
ACT = mybir.ActivationFunctionType
ALU = mybir.AluOpType

P = 128
PACK = 4
K_PASS = P * PACK

TOKENS = 128
D = 512
LEAVES = 16
NODES = LEAVES - 1
F = 64
PASSES = LEAVES * F // K_PASS
PASS_LEAVES = LEAVES // PASSES
PAIR = 2
TOKEN_RUN = 4
BIAS_COL = 64
RUN = 4
CHUNKS = 4
F_PAIRS = F // PAIR
HALVES = 2
E_HALF = D // HALVES
PIECES = ((0, 256), (256, 384), (384, 512))
T_HALF = PACK // HALVES
LOAD_LEAVES = PASS_LEAVES // HALVES

FLOPS = 2 * TOKENS * D * LEAVES * F * 2


def tile_fastfeedforwardnetwork_pa_s_kernel(tc, x, node_logits, node_b, w1, b1, w2, out):
    nc = tc.nc
    assert D == K_PASS and TOKENS == P
    with ExitStack() as ctx:
        keep = ctx.enter_context(tc.tile_pool(name="keep", bufs=1))
        psum = ctx.enter_context(tc.psum_pool(name="psum", bufs=1))
        ctx.enter_context(tc.manual_schedule())

        gate_rows = keep.tile([P, BIAS_COL + NODES + 1], BF16)
        nc.vector.memset(gate_rows[:], 0.0)
        x_rows = keep.tile([P, D], BF16)
        w1_raw = [
            [keep.tile([P, LOAD_LEAVES, PACK * F], BF16, name="w1_raw%d_%d" % (c, part)) for part in range(HALVES)]
            for c in range(PASSES)
        ]
        w2_rows = w2.rearrange("l f e -> (l f) e")
        w2_raw = [keep.tile([P, PACK, D], BF16, name="w2_raw%d" % c) for c in range(PASSES)]
        b1_rows = keep.tile([P, P * PAIR], BF16)

        def load_gates():
            nc.sync.dma_start(out=gate_rows[0:1, BIAS_COL : BIAS_COL + NODES], in_=node_b.unsqueeze(0))
            nc.sync.dma_start(
                out=gate_rows[0 : TOKENS // TOKEN_RUN, 0 : TOKEN_RUN * NODES],
                in_=node_logits.rearrange("b t n -> (b t n)").rearrange("(q s) -> q s", s=TOKEN_RUN * NODES),
            )

        def load_x():
            nc.sync.dma_start(out=x_rows[:], in_=x.flatten_outer_dims())

        def load_w1(c, part):
            first = c * PASS_LEAVES + part * LOAD_LEAVES
            nc.sync.dma_start(
                out=w1_raw[c][part][:],
                in_=w1[first : first + LOAD_LEAVES].rearrange("l (p j) f -> p l (j f)", j=PACK),
            )

        def load_w2(c):
            k_rows = slice(c * K_PASS, (c + 1) * K_PASS)
            nc.sync.dma_start(out=w2_raw[c][:].rearrange("p (u e) n -> p u (e n)", u=HALVES), in_=w2_rows[k_rows].rearrange("(u p e) n -> p u (e n)", u=HALVES, e=PAIR))

        def load_b1():
            nc.vector.memset(b1_rows[:], 0.0)
            nc.scalar.dma_start(
                out=b1_rows[0:CHUNKS, :],
                in_=b1.rearrange("l f -> (l f)").rearrange("(q n) -> q n", q=CHUNKS),
            )

        load_b1()
        load_w1(0, 0)
        load_x()
        load_gates()
        load_w1(0, 1)
        for part in range(HALVES):
            load_w1(1, part)
        for c in range(PASSES):
            load_w2(c)

        identity = keep.tile([P, P], F32)
        nc.vector.memset(identity[:], 0.0)
        make_identity(nc, identity[:], nomemset=True)
        spread = keep.tile([P, TOKEN_RUN, TOKENS], BF16)
        nc.vector.memset(spread[:], 0.0)
        nc.gpsimd.affine_select(
            out=spread[:],
            in_=spread[:],
            compare_op=ALU.not_equal,
            fill=1.0,
            base=0,
            pattern=[[-1, TOKEN_RUN], [1, TOKENS]],
            channel_multiplier=-TOKEN_RUN,
        )
        ones = keep.tile([P, P], BF16)
        nc.vector.memset(ones[:], 1.0)

        x_grouped = keep.tile([P, TOKENS * PACK], BF16, align_bytes=64)
        x_codes = keep.tile([P, TOKENS], U32, align_bytes=64)
        x_scales = keep.tile([P, TOKENS], U8, align_bytes=64)
        w1_grouped = [
            [keep.tile([P, PAIR, P, PACK], BF16, name="w1_grouped%d_%d" % (c, u), align_bytes=64) for u in range(HALVES)]
            for c in range(PASSES)
        ]
        w1_codes = keep.tile([P, PASSES, PACK, P], U32, align_bytes=64)
        w1_scales = keep.tile([P, PASSES, PACK, P], U8, align_bytes=64)
        pre_h = [
            [psum.tile([P, T_HALF, TOKENS], F32, name="pre_h%d_%d" % (c, half)) for half in range(HALVES)]
            for c in range(PASSES)
        ]
        relu_h = [keep.tile([P, PACK, TOKENS], F32, name="relu_h%d" % c) for c in range(PASSES)]
        h_grouped = [keep.tile([P, TOKENS, PACK], BF16, name="h_grouped%d" % c, align_bytes=64) for c in range(PASSES)]
        h_codes = keep.tile([P, PASSES, TOKENS], U32, align_bytes=64)
        h_scales = keep.tile([P, PASSES, TOKENS], U8, align_bytes=64)
        w2_grouped = [keep.tile([P, D, PACK], BF16, name="w2_grouped%d" % c, align_bytes=64) for c in range(PASSES)]
        w2_codes = keep.tile([P, PASSES, D], U32, align_bytes=64)
        w2_scales = keep.tile([P, PASSES, D], U8, align_bytes=64)

        def regroup_w1(c, u):
            source = w1_raw[c][u][:].rearrange("p l (j i e) -> p l i j e", j=PACK, e=PAIR)
            target = w1_grouped[c][u][:].rearrange("p e (l i) j -> p l i j e", l=LOAD_LEAVES)
            vector_leaves = LOAD_LEAVES // HALVES
            nc.vector.tensor_copy(out=target[:, 0:vector_leaves], in_=source[:, 0:vector_leaves])
            nc.scalar.copy(out=target[:, vector_leaves:], in_=source[:, vector_leaves:])

        def quantise_w1(c, u):
            ts = slice(u * PAIR, (u + 1) * PAIR)
            nc.vector.quantize_mx(
                out=w1_codes[:, c, ts, :].rearrange("p t m -> p (t m)").bitcast(FP8X4),
                scales=w1_scales[:, c, ts, :].rearrange("p t m -> p (t m)"),
                in_=w1_grouped[c][u][:].rearrange("p e m j -> p (e m j)"),
            )

        def hidden_products(c, u):
            for e in range(PAIR):
                t = PAIR * u + e
                nc.tensor.matmul_mx(
                    out=pre_h[c][u][:, e, :],
                    lhsT=w1_codes[:, c, t, :].bitcast(FP8X4),
                    lhsT_scale=w1_scales[:, c, t, :],
                    rhs=x_codes[:].bitcast(FP8X4),
                    rhs_scale=x_scales[:],
                    start=True,
                    stop=True,
                )

        def bias_relu(c, u):
            for e in range(PAIR):
                nc.scalar.activation(
                    out=relu_h[c][:, PAIR * u + e, :],
                    in_=pre_h[c][u][:, e, :],
                    func=ACT.Relu,
                    bias=b1_cols[:, HALVES * c + u, e : e + 1],
                    scale=1.0,
                )

        def weight_hidden(c):
            nc.vector.tensor_tensor(
                out=h_grouped[c][:].rearrange("p r (u e) -> p r u e", u=HALVES),
                in0=relu_h[c][:].rearrange("p (u e) r -> p r u e", u=HALVES),
                in1=probs_t[:, HALVES * c : HALVES * (c + 1), :]
                .rearrange("p u r -> p r u")
                .unsqueeze(3)
                .to_broadcast([P, TOKENS, HALVES, PAIR]),
                op=ALU.mult,
            )

        def quantise_hidden(c):
            nc.vector.quantize_mx(
                out=h_codes[:, c, :].bitcast(FP8X4),
                scales=h_scales[:, c, :],
                in_=h_grouped[c][:].rearrange("p r t -> p (r t)"),
            )

        def regroup_w2(c):
            source = w2_raw[c][:].rearrange("p t (g i) -> p g t i", i=4)
            target = w2_grouped[c][:].rearrange("p (g i) t -> p g t i", i=4)
            groups = E_HALF // 4
            nc.vector.tensor_copy(out=target[:, 0:groups], in_=source[:, 0:groups])
            nc.scalar.copy(out=target[:, groups : 2 * groups], in_=source[:, groups : 2 * groups])

        def quantise_w2(c, piece):
            e_cols = slice(*PIECES[piece])
            nc.vector.quantize_mx(
                out=w2_codes[:, c, e_cols].bitcast(FP8X4),
                scales=w2_scales[:, c, e_cols],
                in_=w2_grouped[c][:, e_cols, :].rearrange("p e t -> p (e t)"),
            )

        def output_product(c, piece):
            e_cols = slice(*PIECES[piece])
            nc.tensor.matmul_mx(
                out=out_ps[piece][:],
                lhsT=h_codes[:, c, :].bitcast(FP8X4),
                lhsT_scale=h_scales[:, c, :],
                rhs=w2_codes[:, c, e_cols].bitcast(FP8X4),
                rhs_scale=w2_scales[:, c, e_cols],
                start=(c == 0),
                stop=(c == PASSES - 1),
            )

        gates = keep.tile([P, 2, NODES], F32)
        upper = keep.tile([P, 2, 2], F32)
        lower = keep.tile([P, 4, 2, 2], F32)
        leaf_probs = keep.tile([P, 4, 4, F_PAIRS], F32)
        leaf_cols = leaf_probs[:].rearrange("p u v r -> p (u v r)")
        x_words = x_rows[:].bitcast(F32).rearrange("r (p u) -> r u p", u=2)
        x_t = psum.tile([P, 2, TOKENS], F32, tag="x_bank", name="x_t")
        small_t = psum.tile([P, P + NODES + 1], F32, tag="out_bank1", name="small_t")
        b1_t = small_t[:, 0:P]
        pre_gate = small_t[:, P : P + NODES]
        b1_cols = keep.tile([P, CHUNKS, PAIR], BF16)
        probs_t = psum.tile([P, CHUNKS, TOKENS], F32)

        def gate_sums():
            for i in range(TOKEN_RUN):
                nc.tensor.matmul(
                    out=pre_gate,
                    lhsT=spread[:, i, :],
                    rhs=gate_rows[:, i * NODES : (i + 1) * NODES],
                    start=(i == 0),
                    stop=False,
                )
            nc.tensor.matmul(
                out=pre_gate, lhsT=ones[:], rhs=gate_rows[:, BIAS_COL : BIAS_COL + NODES], start=False, stop=True
            )

        def gate_sigmoids():
            nc.scalar.activation(out=gates[:, 0, :], in_=pre_gate, func=ACT.Sigmoid)
            nc.scalar.activation(out=gates[:, 1, :], in_=pre_gate, func=ACT.Sigmoid, scale=-1.0)

        def level_products():
            nc.vector.tensor_tensor(
                out=upper[:],
                in0=gates[:, :, 0].unsqueeze(2).to_broadcast([P, 2, 2]),
                in1=gates[:, :, 1:3].rearrange("p s n -> p n s"),
                op=ALU.mult,
            )
            nc.vector.tensor_tensor(
                out=lower[:],
                in0=gates[:, :, 3:7].rearrange("p s n -> p n s").unsqueeze(3).to_broadcast([P, 4, 2, 2]),
                in1=gates[:, :, 7:15].rearrange("p s (n a) -> p n a s", a=2),
                op=ALU.mult,
            )

        def leaf_products():
            for q in range(CHUNKS):
                nc.vector.tensor_scalar(
                    out=leaf_probs[:, q],
                    in0=lower[:, q].rearrange("p a s -> p (a s)").unsqueeze(2).to_broadcast([P, 4, F_PAIRS]),
                    scalar1=upper[:].rearrange("p n s -> p (n s)")[:, q : q + 1],
                    scalar2=None,
                    op0=ALU.mult,
                )

        def transpose_x():
            for u in range(2):
                nc.tensor.transpose(out=x_t[:, u, :], in_=x_words[:, u, :], identity=identity[:])

        def transpose_b1():
            nc.tensor.transpose(out=b1_t, in_=b1_rows[:].bitcast(F32), identity=identity[:])

        def keep_b1():
            nc.scalar.copy(out=b1_cols[:].rearrange("p q e -> p (q e)").bitcast(F32), in_=b1_t[:, 0:CHUNKS])

        def transpose_probs():
            for chunk in range(CHUNKS):
                nc.tensor.transpose(
                    out=probs_t[:, chunk, :], in_=leaf_cols[:, chunk * P : (chunk + 1) * P], identity=identity[:]
                )

        def group_x():
            nc.vector.tensor_copy(
                out=x_grouped[:].bitcast(F32).rearrange("p (g i u) -> p g u i", i=RUN, u=2),
                in_=x_t[:].rearrange("p u (g i) -> p g u i", i=RUN),
            )

        def quantise_x():
            nc.vector.quantize_mx(out=x_codes[:].bitcast(FP8X4), scales=x_scales[:], in_=x_grouped[:])

        warm = keep.tile([P, 1], F32)
        nc.vector.memset(warm[:], 0.0)
        nc.scalar.activation(out=warm[:], in_=warm[:], func=ACT.Sigmoid)
        regroup_w1(0, 0)
        transpose_x()
        transpose_b1()
        gate_sums()
        quantise_w1(0, 0)
        group_x()
        regroup_w1(0, 1)
        gate_sigmoids()
        keep_b1()
        quantise_x()
        hidden_products(0, 0)
        quantise_w1(0, 1)
        hidden_products(0, 1)
        level_products()
        regroup_w1(1, 0)
        leaf_products()
        transpose_probs()
        bias_relu(0, 0)
        regroup_w1(1, 1)
        bias_relu(0, 1)
        for u in range(HALVES):
            quantise_w1(1, u)
            hidden_products(1, u)
        regroup_w2(0)
        weight_hidden(0)
        for u in range(HALVES):
            bias_relu(1, u)
        regroup_w2(1)

        banks = ("out_bank0", "out_bank1", "x_bank")
        out_ps = [
            psum.tile([P, stop - first], F32, tag=bank, name="out_ps_%s" % bank)
            for (first, stop), bank in zip(PIECES, banks)
        ]
        quantise_w2(0, 0)
        quantise_hidden(0)
        output_product(0, 0)
        for piece in (1, 2):
            quantise_w2(0, piece)
            output_product(0, piece)
        weight_hidden(1)
        quantise_w2(1, 0)
        quantise_hidden(1)
        output_product(1, 0)
        for piece in (1, 2):
            quantise_w2(1, piece)
            output_product(1, piece)

        out_rows = out.flatten_outer_dims()
        result = [keep.tile([P, stop - first], F32, name="result%d" % first) for first, stop in PIECES]
        nc.vector.tensor_copy(out=result[0][:], in_=out_ps[0][:])
        nc.scalar.copy(out=result[1][:], in_=out_ps[1][:])
        nc.vector.tensor_copy(out=result[2][:], in_=out_ps[2][:])
        for piece, (first, stop) in enumerate(PIECES):
            nc.sync.dma_start(out=out_rows[:, first:stop], in_=result[piece][:])
